import numpy as np
import ml_dtypes


def mxq(x, axis, fmt="e4m3"):
    dtype, down = {"e4m3": (ml_dtypes.float8_e4m3fn, 7), "e5m2": (ml_dtypes.float8_e5m2, 14)}[fmt]
    v = np.moveaxis(np.asarray(x, np.float32).astype(ml_dtypes.bfloat16).astype(np.float64), axis, -1)
    blocks = v.reshape(v.shape[:-1] + (-1, 32))
    amax = np.abs(blocks).max(-1, keepdims=True)
    byte = np.maximum(np.where(amax > 0, np.frexp(amax)[1] - 1 + 127, 0) - down, 1)
    scale = np.exp2(byte - 127.0)
    codes = (blocks / scale).astype(np.float32).astype(dtype).astype(np.float64)
    return np.moveaxis((codes * scale).reshape(v.shape), -1, axis)


WIDE = False


def mx_kscale(k):
    if not WIDE:
        return np.ones(k)
    levels = np.array([10, -10, 5, -5, 0])
    if k % 512:
        return np.exp2(np.random.permutation(np.resize(levels, k // 32))).repeat(32)
    a = np.empty((k // 512, 16))
    for p in range(k // 512):
        a[p, :8] = np.random.permutation(np.resize(levels, 8))
        for g in range(8):
            far = levels[np.abs(levels - a[p, g]) >= 10]
            a[p, g + 8] = far[np.random.randint(len(far))]
    return np.exp2(a.ravel()).repeat(32)


BF16 = ml_dtypes.bfloat16


def bf(x):
    return np.asarray(x, np.float32).astype(BF16)


def f64(x):
    return np.asarray(x).astype(np.float64)


B, H, P, D, NF, DO, G = 2, 12, 32, 512, 8, 512, 5
N = D * H * P


def setup_inputs():
    s = mx_kscale(D)
    return {
        "x": bf(np.random.standard_normal((B, H, P, D)) * s),
        "lin_w": bf(np.random.standard_normal((G * D, D)) * 0.3 / np.sqrt(D) / s),
        "lin_b": bf(np.random.standard_normal(G * D) * 0.1),
        "grid": bf(np.arange(NF)[None, :] + 1.0 + 0.1 * np.random.standard_normal((G, NF))),
        "coef": bf(np.random.standard_normal((N, NF, G)) * 0.5),
        "shift": bf(np.random.standard_normal((1, H, G, P, D)) * 0.5),
    }


def core(x, lin_w, lin_b, grid, coef, shift):
    xl = (mxq(f64(x), 3, "e4m3") @ mxq(f64(lin_w).T, 0, "e4m3")) + f64(lin_b)
    xl = xl.reshape(B, G, N)
    sn = np.sin(f64(grid)[None, :, :, None] * xl[:, :, None, :])
    f = sn * f64(coef).transpose(2, 1, 0)[None]
    return f.reshape(B, H, G, NF, P, D).sum(axis=3) + f64(shift)


def e4m3fn_bytes(y):
    return np.clip(np.asarray(y, np.float64), -448.0, 448.0).astype(np.float32).astype(ml_dtypes.float8_e4m3fn).view(np.uint8)


def reference(x, lin_w, lin_b, grid, coef, shift):
    out = core(x, lin_w, lin_b, grid, coef, shift)
    s = np.max(np.abs(out), axis=-1, keepdims=True) / 448.0
    return out, e4m3fn_bytes(out / s)

@@ -1,0 +1,408 @@
+from contextlib import ExitStack
+
+import concourse.mybir as mybir
+from concourse.masks import make_identity
+
+FLOPS = 2 * 768 * 2560 * 512
+
+F32 = mybir.dt.float32
+BF16 = mybir.dt.bfloat16
+I32 = mybir.dt.int32
+U32 = mybir.dt.uint32
+U8 = mybir.dt.uint8
+FP8X4 = mybir.dt.float8_e4m3fn_x4
+FP8 = mybir.dt.float8_e4m3fn
+ALU = mybir.AluOpType
+ACT = mybir.ActivationFunctionType
+AX = mybir.AxisListType
+
+P = 128
+MANUAL = True
+TWO_PI = 6.283185307179586
+
+
+def tile_ka_attention_heads_mod_pa_kernel(tc, x, lin_w, lin_b, grid, coef, shift, out_0, out_1):
+    nc = tc.nc
+    with ExitStack() as ctx:
+        const = ctx.enter_context(tc.tile_pool(name="const", bufs=1))
+        coefp = ctx.enter_context(tc.tile_pool(name="coefp", bufs=1))
+
+        ident_f = const.tile([P, P], F32, name="ident_f")
+        make_identity(nc, ident_f[:])
+        ident_b = const.tile([P, P], BF16, name="ident_b")
+        make_identity(nc, ident_b[:])
+        zero_col = const.tile([P, 1], F32, name="zero_col")
+        nc.vector.memset(zero_col[:], 0.0)
+        warm = const.tile([P, 1], F32, name="warm")
+        nc.scalar.activation(out=warm[:], in_=zero_col[:], func=ACT.Sin)
+
+        wc = const.tile([P, 2560], U32, name="wc", align_bytes=64)
+        ws = const.tile([P, 2560], U8, name="ws", align_bytes=64)
+        xc = const.tile([P, 768], U32, name="xc", align_bytes=64)
+        xs = const.tile([P, 768], U8, name="xs", align_bytes=64)
+        gsc = const.tile([P, 40], F32, name="gsc")
+        bias_t = const.tile([P, 20], F32, name="bias_t")
+
+        cn = {}
+        coef_v = coef.rearrange("(r d) m j -> r d (m j)", d=512)
+
+        with ExitStack() as setup:
+            stage = setup.enter_context(tc.tile_pool(name="stage", bufs=1))
+            pss = setup.enter_context(tc.psum_pool(name="pss", bufs=3))
+
+            x_sb = stage.tile([P, 6, 512], BF16, name="x_sb")
+            nc.sync.dma_start(
+                out=x_sb[:],
+                in_=x.rearrange("b h p d -> (b h p) d").rearrange("(t p) d -> p t d", p=P),
+            )
+            lb = stage.tile([P, P], BF16, name="lb")
+            nc.vector.memset(lb[:], 0.0)
+            nc.sync.dma_start(out=lb[0:20, :], in_=lin_b.rearrange("(t p) -> t p", p=P))
+            gb = stage.tile([P, 40], BF16, name="gb")
+            nc.sync.dma_start(out=gb[:], in_=grid.rearrange("g f -> (g f)").partition_broadcast(P))
+            w_sb = stage.tile([P, 20, 512], BF16, name="w_sb")
+            w_v = lin_w.rearrange("(t p) k -> p t k", p=P)
+            for cc in range(5):
+                nc.sync.dma_start(out=w_sb[:, 4 * cc : 4 * cc + 4, :], in_=w_v[:, 4 * cc : 4 * cc + 4, :])
+            for kap in range(3):
+                for dc in range(4):
+                    cn[(kap, dc)] = coefp.tile([P, P, 40], BF16, name="cn%d_%d" % (kap, dc))
+                    nc.sync.dma_start(
+                        out=cn[(kap, dc)][:],
+                        in_=coef_v[kap * P : (kap + 1) * P, dc * P : (dc + 1) * P, :],
+                    )
+
+            nc.vector.tensor_scalar(out=gsc[:], in0=gb[:], scalar1=1.0 / TWO_PI, scalar2=None, op0=ALU.mult)
+            tb = pss.tile([P, P], BF16, name="tb", bufs=1)
+            nc.tensor.transpose(tb[:], lb[:], ident_b[:])
+            nc.vector.tensor_copy(out=bias_t[:], in_=tb[:, 0:20])
+
+            gx = stage.tile([P, 768, 4], BF16, name="gx", align_bytes=64)
+            gw = stage.tile([P, 2560, 4], BF16, name="gw", align_bytes=64)
+
+            def turn(words, t_lo, t_hi, grouped32):
+                for t0 in range(t_lo, t_hi, 2):
+                    tp = pss.tile([P, 2, 2, P], F32, name="tp")
+                    for e in range(2):
+                        for u in range(2):
+                            nc.tensor.transpose(tp[:, e, u, :], words[:, t0 + e, u:256:2], ident_f[:])
+                    dst = grouped32[:, t0 * P : (t0 + 2) * P, :].rearrange("p (e r) u -> p e r u", e=2)
+                    src = tp[:].rearrange("p e u r -> p e r u")
+                    if (t0 // 2) % 2 == 0:
+                        nc.vector.tensor_copy(out=dst, in_=src)
+                    else:
+                        nc.scalar.copy(out=dst, in_=src)
+
+            def quant(grouped, codes, scales, lo, hi):
+                nc.vector.quantize_mx(
+                    out=codes[:, lo:hi].bitcast(FP8X4),
+                    scales=scales[:, lo:hi],
+                    in_=grouped[:, lo:hi, :].rearrange("p r t -> p (r t)"),
+                )
+
+            x_words = x_sb[:].bitcast(F32)
+            w_words = w_sb[:].bitcast(F32)
+            gx32 = gx[:].bitcast(F32)
+            gw32 = gw[:].bitcast(F32)
+            turn(x_words, 0, 6, gx32)
+            turn(w_words, 0, 4, gw32)
+            quant(gx, xc, xs, 0, 512)
+            quant(gx, xc, xs, 512, 768)
+            for cc in range(1, 5):
+                turn(w_words, 4 * cc, 4 * cc + 4, gw32)
+                quant(gw, wc, ws, 512 * (cc - 1), 512 * cc)
+            quant(gw, wc, ws, 2048, 2560)
+
+        xpool = ctx.enter_context(tc.tile_pool(name="xpool", bufs=2))
+        tpool = ctx.enter_context(tc.tile_pool(name="tpool", bufs=1))
+        kpool = ctx.enter_context(tc.tile_pool(name="kpool", bufs=1))
+        spool = ctx.enter_context(tc.tile_pool(name="spool", bufs=2))
+        ppool = ctx.enter_context(tc.tile_pool(name="ppool", bufs=3))
+        opool = ctx.enter_context(tc.tile_pool(name="opool", bufs=2))
+        psa = ctx.enter_context(tc.psum_pool(name="psa", bufs=2))
+        psc = ctx.enter_context(tc.psum_pool(name="psc", bufs=4))
+        psx = ctx.enter_context(tc.psum_pool(name="psx", bufs=2))
+        if MANUAL:
+            ctx.enter_context(tc.manual_schedule())
+
+        out0_v = out_0.rearrange("b h g p d -> b (h g p) d")
+        out1_v = out_1.rearrange("b h g p d -> b (h g p) d")
+        shift_v = shift.rearrange("o h g p d -> (o h g p) d")
+
+        xt = {}
+        xq_of = {}
+        kt_of = {}
+        s_of = {}
+        ct_of = {}
+        pt = {}
+        sh_of = {}
+        cts_of = {}
+        sht_of = {}
+        acc_of = {}
+        cur = {}
+
+        def xmm(t):
+            xq_of[t] = psx.tile([P, 2, 2, P], F32, name="xq")
+            for e in range(2):
+                dc, cc = divmod(2 * t + e, 5)
+                ch = (cc * 4 + dc) * P
+                for b in range(2):
+                    col = b * 384 + cur["c0"] * 64
+                    nc.tensor.matmul_mx(
+                        out=xq_of[t][:, e, b, :],
+                        lhsT=wc[:, ch : ch + P].bitcast(FP8X4),
+                        lhsT_scale=ws[:, ch : ch + P],
+                        rhs=xc[:, col : col + P].bitcast(FP8X4),
+                        rhs_scale=xs[:, col : col + P],
+                        start=True,
+                        stop=True,
+                    )
+
+        def x_geometry(j):
+            r_lo = (384 * j) // 5
+            cur["n"] = (384 * j + 383) // 5 + 1 - r_lo
+            cur["c0"] = r_lo // 64
+            cur["a"] = r_lo - 64 * cur["c0"]
+
+        def xev(j, t, first):
+            n = cur["n"]
+            a = cur["a"]
+            if t == 0:
+                xt[j] = xpool.tile([P, 2, 4, 390], F32, name="xt")
+            for e in range(2):
+                dc, cc = divmod(2 * t + e, 5)
+                if cc == 0:
+                    cur["tmp"] = tpool.tile([P, 5, 2, 78], F32, name="tmp")
+                if first and e == 1:
+                    nc.vector.tensor_scalar(
+                        out=cur["tmp"][:, cc, :, 0:n],
+                        in0=xq_of[t][:, e, :, a : a + n],
+                        scalar1=bias_t[:, cc * 4 + dc : cc * 4 + dc + 1],
+                        scalar2=None,
+                        op0=ALU.add,
+                    )
+                else:
+                    nc.scalar.activation(
+                        out=cur["tmp"][:, cc, :, 0:n],
+                        in_=xq_of[t][:, e, :, a : a + n],
+                        func=ACT.Identity,
+                        bias=bias_t[:, cc * 4 + dc : cc * 4 + dc + 1],
+                        scale=1.0,
+                    )
+                if cc == 4:
+                    dst = xt[j][:, :, dc, 0 : 5 * n].rearrange("p b (r c) -> p b r c", c=5)
+                    src = cur["tmp"][:, :, :, 0:n].rearrange("p c b r -> p b r c")
+                    if first:
+                        nc.vector.tensor_copy(out=dst, in_=src)
+                    else:
+                        nc.scalar.copy(out=dst, in_=src)
+
+        def x_slice(s, b):
+            j = s // 8
+            o = 384 * j - 5 * ((384 * j) // 5)
+            return xt[j][:, b, :, o : o + 384]
+
+        def do_k(s):
+            eng = nc.vector if s == 0 else nc.gpsimd
+            for b in range(2):
+                kt_of[(s, b)] = kpool.tile([P, 4, 384], I32, name="kt%d" % b)
+                eng.tensor_scalar(
+                    out=kt_of[(s, b)][:],
+                    in0=x_slice(s, b),
+                    scalar1=gsc[:, s : s + 1],
+                    scalar2=0.0,
+                    op0=ALU.mult,
+                    op1=ALU.add,
+                )
+
+        def do_r(s):
+            s_of[s] = spool.tile([P, 2, 4, 384], F32, name="st")
+            for b in range(2):
+                nc.vector.scalar_tensor_tensor(
+                    out=s_of[s][:, b],
+                    in0=x_slice(s, b),
+                    scalar=gsc[:, s : s + 1],
+                    in1=kt_of[(s, b)][:],
+                    op0=ALU.mult,
+                    op1=ALU.subtract,
+                )
+            for b in range(2):
+                nc.scalar.activation(out=s_of[s][:, b], in_=s_of[s][:, b], func=ACT.Sin, scale=TWO_PI)
+
+        def do_ct(g):
+            j, q = divmod(g, 24)
+            m, kap = divmod(q, 3)
+            ct_of[g] = psc.tile([P, 4, P], BF16, name="ct")
+            for dc in range(4):
+                nc.tensor.transpose(ct_of[g][:, dc, :], cn[(kap, dc)][:, :, m * 5 + j], ident_b[:])
+
+        def do_m(g):
+            j, q = divmod(g, 24)
+            m, kap = divmod(q, 3)
+            sel = (q % 4) // 2
+            h = q % 2
+            if sel == 0:
+                pt[h] = ppool.tile([P, 4, 4, 4, 32], F32, name="pt")
+            nc.vector.tensor_tensor(
+                out=pt[h][:].rearrange("p c i (b s) q -> p b c i s q", b=2)[:, :, :, :, sel, :],
+                in0=s_of[j * 8 + m][:, :, :, kap * P : (kap + 1) * P].rearrange("p b c (i q) -> p b c i q", i=4),
+                in1=ct_of[g][:].rearrange("p c (i q) -> p c i q", i=4).unsqueeze(1).to_broadcast([P, 2, 4, 4, 32]),
+                op=ALU.mult,
+            )
+
+        def sh_load(n):
+            sh_of[n] = opool.tile([P, 512], BF16, name="sh")
+            for b in range(2):
+                nc.sync.dma_start(out=sh_of[n][b * 64 : (b + 1) * 64, :], in_=shift_v[n * 64 : (n + 1) * 64, :])
+
+        def sh_turn(n):
+            cts_of[n] = psc.tile([P, 4, P], BF16, name="ct")
+            for dc in range(4):
+                nc.tensor.transpose(cts_of[n][:, dc, :], sh_of[n][:, dc * P : (dc + 1) * P], ident_b[:])
+
+        def sh_copy(n):
+            def run():
+                sht_of[n] = opool.tile([P, 4, P], F32, name="sht")
+                nc.scalar.copy(out=sht_of[n][:], in_=cts_of[n][:])
+
+            return run
+
+        def do_ta(n, h):
+            if h == 0:
+                acc_of[n] = psa.tile([P, 512], F32, name="acc")
+                for dc in range(4):
+                    nc.tensor.matmul(
+                        out=acc_of[n][:, dc * P : (dc + 1) * P],
+                        lhsT=sht_of[n][:, dc, :],
+                        rhs=ident_f[:],
+                        is_transpose=True,
+                        start=(dc == 0),
+                        stop=False,
+                    )
+            for dc in range(4):
+                for i in range(4):
+                    nc.tensor.matmul(
+                        out=acc_of[n][:, dc * P : (dc + 1) * P],
+                        lhsT=pt[h][:, dc, i].rearrange("p a q -> p (a q)"),
+                        rhs=ident_f[:],
+                        is_transpose=True,
+                        start=False,
+                        stop=(h == 1 and dc == 3 and i == 3),
+                    )
+
+        def out_chain(n):
+            t = {}
+            rows = slice(n * 64, (n + 1) * 64)
+
+            def evac():
+                t["o"] = opool.tile([P, 512], F32, name="o")
+                nc.scalar.copy(out=t["o"][:], in_=acc_of[n][:])
+                for b in range(2):
+                    nc.sync.dma_start(out=out0_v[b, rows, :], in_=t["o"][b * 64 : (b + 1) * 64, :])
+
+            def amax():
+                t["am"] = opool.tile([P, 1], F32, name="am")
+                nc.vector.tensor_reduce(
+                    out=t["am"][:], in_=t["o"][:], axis=AX.X, op=ALU.max, apply_absolute_value=True
+                )
+
+            def recip():
+                t["rc"] = opool.tile([P, 1], F32, name="rc")
+                nc.vector.reciprocal(out=t["rc"][:], in_=t["am"][:])
+
+            def cast():
+                t["rs"] = opool.tile([P, 1], F32, name="rs")
+                nc.scalar.activation(out=t["rs"][:], in_=t["rc"][:], func=ACT.Copy, scale=448.0)
+                t["f8"] = opool.tile([P, 512], FP8, name="f8")
+                nc.scalar.activation(
+                    out=t["f8"][:],
+                    in_=t["o"][:],
+                    func=ACT.Identity,
+                    scale=t["rs"][:, 0:1],
+                    bias=zero_col[:, 0:1],
+                    saturate=False,
+                )
+                nc.sync.dma_start(out=out1_v[:, rows, :], in_=t["f8"][:].bitcast(U8))
+
+            return evac, amax, recip, cast
+
+        def xev_later(j, t):
+            def run():
+                xev(j, t, False)
+
+            return run
+
+        sh_load(0)
+        sh_load(1)
+        x_geometry(0)
+        xmm(0)
+        for t in range(10):
+            if t + 1 < 10:
+                xmm(t + 1)
+            xev(0, t, True)
+        do_k(0)
+        do_r(0)
+        do_k(1)
+        sh_turn(0)
+        sh_copy(0)()
+        do_ct(0)
+        do_ct(1)
+
+        casts = []
+        evacs = []
+        copies = []
+        xevs = []
+        dve_small = []
+        for s in range(40):
+            j, m = divmod(s, 8)
+            for fn in casts:
+                fn()
+            new_small = []
+            for fns in evacs:
+                fns[0]()
+                new_small.extend([fns[1], fns[2]])
+            cast_next = [fns[3] for fns in evacs]
+            for fn in copies + xevs:
+                fn()
+            casts = cast_next
+            evacs = []
+            copies = []
+            xevs = []
+            dve_small.extend(new_small)
+            if s + 1 < 40:
+                do_r(s + 1)
+            if s + 2 < 40:
+                do_k(s + 2)
+            for kap in range(3):
+                g = 3 * s + kap
+                if g + 2 < 120:
+                    do_ct(g + 2)
+                if g >= 1 and (g - 1) % 4 >= 2:
+                    do_ta((g - 1) // 4, (g - 1) % 2)
+                    if (g - 1) % 4 == 3:
+                        evacs.extend([out_chain((g - 1) // 4)])
+                if g % 4 == 0 and g // 4 + 1 < 30:
+                    sh_turn(g // 4 + 1)
+                    copies.extend([sh_copy(g // 4 + 1)])
+                    if g // 4 + 2 < 30:
+                        sh_load(g // 4 + 2)
+                do_m(g)
+                if dve_small:
+                    dve_small[0]()
+                    dve_small = dve_small[1:]
+            if j < 4 and m <= 4:
+                if m == 0:
+                    x_geometry(j + 1)
+                for t in (2 * m, 2 * m + 1):
+                    xmm(t)
+                    xevs.extend([xev_later(j + 1, t)])
+        do_ta(29, 1)
+        last = out_chain(29)
+        for fn in dve_small:
+            fn()
+        for fn in casts:
+            fn()
+        last[0]()
+        last[1]()
+        last[2]()
+        last[3]()

@@ -58,8 +58,12 @@ def tile_ka_attention_heads_mod_pa_kernel(tc, x, lin_w, lin_b, grid, coef, shift
             lb = stage.tile([P, P], BF16, name="lb")
             nc.vector.memset(lb[:], 0.0)
             nc.sync.dma_start(out=lb[0:20, :], in_=lin_b.rearrange("(t p) -> t p", p=P))
-            gb = stage.tile([P, 40], BF16, name="gb")
-            nc.sync.dma_start(out=gb[:], in_=grid.rearrange("g f -> (g f)").partition_broadcast(P))
+            g_row = stage.tile([P, 40], BF16, name="g_row")
+            nc.vector.memset(g_row[:], 0.0)
+            nc.sync.dma_start(out=g_row[0:1, :], in_=grid.rearrange("(o g) f -> o (g f)", o=1))
+            first_row = stage.tile([P, P], BF16, name="first_row")
+            nc.vector.memset(first_row[:], 0.0)
+            nc.vector.memset(first_row[0:1, :], 1.0)
             w_sb = stage.tile([P, 20, 512], BF16, name="w_sb")
             w_v = lin_w.rearrange("(t p) k -> p t k", p=P)
             for cc in range(5):
@@ -72,10 +76,12 @@ def tile_ka_attention_heads_mod_pa_kernel(tc, x, lin_w, lin_b, grid, coef, shift
                         in_=coef_v[kap * P : (kap + 1) * P, dc * P : (dc + 1) * P, :],
                     )
 
-            nc.vector.tensor_scalar(out=gsc[:], in0=gb[:], scalar1=1.0 / TWO_PI, scalar2=None, op0=ALU.mult)
             tb = pss.tile([P, P], BF16, name="tb", bufs=1)
             nc.tensor.transpose(tb[:], lb[:], ident_b[:])
             nc.vector.tensor_copy(out=bias_t[:], in_=tb[:, 0:20])
+            gp = pss.tile([P, 40], F32, name="tb", bufs=1)
+            nc.tensor.matmul(out=gp[:], lhsT=first_row[:], rhs=g_row[:], start=True, stop=True)
+            nc.vector.tensor_scalar(out=gsc[:], in0=gp[:], scalar1=1.0 / TWO_PI, scalar2=None, op0=ALU.mult)
 
             gx = stage.tile([P, 768, 4], BF16, name="gx", align_bytes=64)
             gw = stage.tile([P, 2560, 4], BF16, name="gw", align_bytes=64)
@@ -343,6 +349,8 @@ def tile_ka_attention_heads_mod_pa_kernel(tc, x, lin_w, lin_b, grid, coef, shift
         do_k(0)
         do_r(0)
         do_k(1)
+        do_r(1)
+        do_k(2)
         sh_turn(0)
         sh_copy(0)()
         do_ct(0)
@@ -369,9 +377,9 @@ def tile_ka_attention_heads_mod_pa_kernel(tc, x, lin_w, lin_b, grid, coef, shift
             copies = []
             xevs = []
             dve_small.extend(new_small)
-            if s + 1 < 40:
+            if s + 1 < 40 and s + 1 not in s_of:
                 do_r(s + 1)
-            if s + 2 < 40:
+            if s + 2 < 40 and (s + 2, 0) not in kt_of:
                 do_k(s + 2)
             for kap in range(3):
                 g = 3 * s + kap

@@ -18,6 +18,11 @@ AX = mybir.AxisListType
 
 P = 128
 MANUAL = True
+
+
+def plain_shift(n):
+    return n % 3 == 0
+
 TWO_PI = 6.283185307179586
 
 
@@ -257,7 +262,7 @@ def tile_ka_attention_heads_mod_pa_kernel(tc, x, lin_w, lin_b, grid, coef, shift
             )
 
         def sh_load(n):
-            sh_of[n] = opool.tile([P, 512], BF16, name="sh")
+            sh_of[n] = opool.tile([P, 512], BF16, name="sh", bufs=3)
             for b in range(2):
                 nc.sync.dma_start(out=sh_of[n][b * 64 : (b + 1) * 64, :], in_=shift_v[n * 64 : (n + 1) * 64, :])
 
@@ -276,7 +281,9 @@ def tile_ka_attention_heads_mod_pa_kernel(tc, x, lin_w, lin_b, grid, coef, shift
         def do_ta(n, h):
             if h == 0:
                 acc_of[n] = psa.tile([P, 512], F32, name="acc")
-                for dc in range(4):
+                if plain_shift(n):
+                    nc.tensor.matmul(out=acc_of[n][:], lhsT=ident_b[:], rhs=sh_of[n][:], start=True, stop=False)
+                for dc in range(0 if plain_shift(n) else 4):
                     nc.tensor.matmul(
                         out=acc_of[n][:, dc * P : (dc + 1) * P],
                         lhsT=sht_of[n][:, dc, :],
@@ -351,8 +358,6 @@ def tile_ka_attention_heads_mod_pa_kernel(tc, x, lin_w, lin_b, grid, coef, shift
         do_k(1)
         do_r(1)
         do_k(2)
-        sh_turn(0)
-        sh_copy(0)()
         do_ct(0)
         do_ct(1)
 
@@ -390,8 +395,9 @@ def tile_ka_attention_heads_mod_pa_kernel(tc, x, lin_w, lin_b, grid, coef, shift
                     if (g - 1) % 4 == 3:
                         evacs.extend([out_chain((g - 1) // 4)])
                 if g % 4 == 0 and g // 4 + 1 < 30:
-                    sh_turn(g // 4 + 1)
-                    copies.extend([sh_copy(g // 4 + 1)])
+                    if not plain_shift(g // 4 + 1):
+                        sh_turn(g // 4 + 1)
+                        copies.extend([sh_copy(g // 4 + 1)])
                     if g // 4 + 2 < 30:
                         sh_load(g // 4 + 2)
                 do_m(g)

@@ -17,13 +17,19 @@ ACT = mybir.ActivationFunctionType
 AX = mybir.AxisListType
 
 P = 128
-MANUAL = True
+HEAD = 4
+TWO_PI = 6.283185307179586
 
 
 def plain_shift(n):
     return n % 3 == 0
 
-TWO_PI = 6.283185307179586
+
+def geometry(j):
+    r_lo = (384 * j) // 5
+    n = (384 * j + 383) // 5 + 1 - r_lo
+    c0 = r_lo // 64
+    return n, c0, r_lo - 64 * c0
 
 
 def tile_ka_attention_heads_mod_pa_kernel(tc, x, lin_w, lin_b, grid, coef, shift, out_0, out_1):
@@ -31,6 +37,15 @@ def tile_ka_attention_heads_mod_pa_kernel(tc, x, lin_w, lin_b, grid, coef, shift
     with ExitStack() as ctx:
         const = ctx.enter_context(tc.tile_pool(name="const", bufs=1))
         coefp = ctx.enter_context(tc.tile_pool(name="coefp", bufs=1))
+        xpool = ctx.enter_context(tc.tile_pool(name="xpool", bufs=2))
+        tpool = ctx.enter_context(tc.tile_pool(name="tpool", bufs=1))
+        kpool = ctx.enter_context(tc.tile_pool(name="kpool", bufs=1))
+        spool = ctx.enter_context(tc.tile_pool(name="spool", bufs=2))
+        ppool = ctx.enter_context(tc.tile_pool(name="ppool", bufs=3))
+        opool = ctx.enter_context(tc.tile_pool(name="opool", bufs=2))
+        psa = ctx.enter_context(tc.psum_pool(name="psa", bufs=2))
+        psc = ctx.enter_context(tc.psum_pool(name="psc", bufs=4))
+        psx = ctx.enter_context(tc.psum_pool(name="psx", bufs=2))
 
         ident_f = const.tile([P, P], F32, name="ident_f")
         make_identity(nc, ident_f[:])
@@ -47,99 +62,24 @@ def tile_ka_attention_heads_mod_pa_kernel(tc, x, lin_w, lin_b, grid, coef, shift
         xs = const.tile([P, 768], U8, name="xs", align_bytes=64)
         gsc = const.tile([P, 40], F32, name="gsc")
         bias_t = const.tile([P, 20], F32, name="bias_t")
+        lb = const.tile([P, P], BF16, name="lb")
+        nc.vector.memset(lb[:], 0.0)
+        g_row = const.tile([P, 40], BF16, name="g_row")
+        nc.vector.memset(g_row[:], 0.0)
+        first_row = const.tile([P, P], BF16, name="first_row")
+        nc.vector.memset(first_row[:], 0.0)
+        nc.vector.memset(first_row[0:1, :], 1.0)
 
-        cn = {}
-        coef_v = coef.rearrange("(r d) m j -> r d (m j)", d=512)
-
-        with ExitStack() as setup:
-            stage = setup.enter_context(tc.tile_pool(name="stage", bufs=1))
-            pss = setup.enter_context(tc.psum_pool(name="pss", bufs=3))
-
-            x_sb = stage.tile([P, 6, 512], BF16, name="x_sb")
-            nc.sync.dma_start(
-                out=x_sb[:],
-                in_=x.rearrange("b h p d -> (b h p) d").rearrange("(t p) d -> p t d", p=P),
-            )
-            lb = stage.tile([P, P], BF16, name="lb")
-            nc.vector.memset(lb[:], 0.0)
-            nc.sync.dma_start(out=lb[0:20, :], in_=lin_b.rearrange("(t p) -> t p", p=P))
-            g_row = stage.tile([P, 40], BF16, name="g_row")
-            nc.vector.memset(g_row[:], 0.0)
-            nc.sync.dma_start(out=g_row[0:1, :], in_=grid.rearrange("(o g) f -> o (g f)", o=1))
-            first_row = stage.tile([P, P], BF16, name="first_row")
-            nc.vector.memset(first_row[:], 0.0)
-            nc.vector.memset(first_row[0:1, :], 1.0)
-            w_sb = stage.tile([P, 20, 512], BF16, name="w_sb")
-            w_v = lin_w.rearrange("(t p) k -> p t k", p=P)
-            for cc in range(5):
-                nc.sync.dma_start(out=w_sb[:, 4 * cc : 4 * cc + 4, :], in_=w_v[:, 4 * cc : 4 * cc + 4, :])
-            for kap in range(3):
-                for dc in range(4):
-                    cn[(kap, dc)] = coefp.tile([P, P, 40], BF16, name="cn%d_%d" % (kap, dc))
-                    nc.sync.dma_start(
-                        out=cn[(kap, dc)][:],
-                        in_=coef_v[kap * P : (kap + 1) * P, dc * P : (dc + 1) * P, :],
-                    )
-
-            tb = pss.tile([P, P], BF16, name="tb", bufs=1)
-            nc.tensor.transpose(tb[:], lb[:], ident_b[:])
-            nc.vector.tensor_copy(out=bias_t[:], in_=tb[:, 0:20])
-            gp = pss.tile([P, 40], F32, name="tb", bufs=1)
-            nc.tensor.matmul(out=gp[:], lhsT=first_row[:], rhs=g_row[:], start=True, stop=True)
-            nc.vector.tensor_scalar(out=gsc[:], in0=gp[:], scalar1=1.0 / TWO_PI, scalar2=None, op0=ALU.mult)
-
-            gx = stage.tile([P, 768, 4], BF16, name="gx", align_bytes=64)
-            gw = stage.tile([P, 2560, 4], BF16, name="gw", align_bytes=64)
-
-            def turn(words, t_lo, t_hi, grouped32):
-                for t0 in range(t_lo, t_hi, 2):
-                    tp = pss.tile([P, 2, 2, P], F32, name="tp")
-                    for e in range(2):
-                        for u in range(2):
-                            nc.tensor.transpose(tp[:, e, u, :], words[:, t0 + e, u:256:2], ident_f[:])
-                    dst = grouped32[:, t0 * P : (t0 + 2) * P, :].rearrange("p (e r) u -> p e r u", e=2)
-                    src = tp[:].rearrange("p e u r -> p e r u")
-                    if (t0 // 2) % 2 == 0:
-                        nc.vector.tensor_copy(out=dst, in_=src)
-                    else:
-                        nc.scalar.copy(out=dst, in_=src)
-
-            def quant(grouped, codes, scales, lo, hi):
-                nc.vector.quantize_mx(
-                    out=codes[:, lo:hi].bitcast(FP8X4),
-                    scales=scales[:, lo:hi],
-                    in_=grouped[:, lo:hi, :].rearrange("p r t -> p (r t)"),
-                )
-
-            x_words = x_sb[:].bitcast(F32)
-            w_words = w_sb[:].bitcast(F32)
-            gx32 = gx[:].bitcast(F32)
-            gw32 = gw[:].bitcast(F32)
-            turn(x_words, 0, 6, gx32)
-            turn(w_words, 0, 4, gw32)
-            quant(gx, xc, xs, 0, 512)
-            quant(gx, xc, xs, 512, 768)
-            for cc in range(1, 5):
-                turn(w_words, 4 * cc, 4 * cc + 4, gw32)
-                quant(gw, wc, ws, 512 * (cc - 1), 512 * cc)
-            quant(gw, wc, ws, 2048, 2560)
-
-        xpool = ctx.enter_context(tc.tile_pool(name="xpool", bufs=2))
-        tpool = ctx.enter_context(tc.tile_pool(name="tpool", bufs=1))
-        kpool = ctx.enter_context(tc.tile_pool(name="kpool", bufs=1))
-        spool = ctx.enter_context(tc.tile_pool(name="spool", bufs=2))
-        ppool = ctx.enter_context(tc.tile_pool(name="ppool", bufs=3))
-        opool = ctx.enter_context(tc.tile_pool(name="opool", bufs=2))
-        psa = ctx.enter_context(tc.psum_pool(name="psa", bufs=2))
-        psc = ctx.enter_context(tc.psum_pool(name="psc", bufs=4))
-        psx = ctx.enter_context(tc.psum_pool(name="psx", bufs=2))
-        if MANUAL:
-            ctx.enter_context(tc.manual_schedule())
+        ctx.enter_context(tc.manual_schedule())
 
         out0_v = out_0.rearrange("b h g p d -> b (h g p) d")
         out1_v = out_1.rearrange("b h g p d -> b (h g p) d")
         shift_v = shift.rearrange("o h g p d -> (o h g p) d")
+        coef_v = coef.rearrange("(r d) m j -> r d (m j)", d=512)
+        x_v = x.rearrange("b h p d -> (b h p) d").rearrange("(t p) d -> p t d", p=P)
+        w_v = lin_w.rearrange("(c q p) k -> p q c k", q=4, p=P)
 
+        cn = {}
         xt = {}
         xq_of = {}
         kt_of = {}
@@ -151,16 +91,83 @@ def tile_ka_attention_heads_mod_pa_kernel(tc, x, lin_w, lin_b, grid, coef, shift
         sht_of = {}
         acc_of = {}
         cur = {}
+        kph = {}
+        sph = {}
+        cth = {}
+        pth = {}
 
-        def xmm(t):
-            xq_of[t] = psx.tile([P, 2, 2, P], F32, name="xq")
+        def load_coef(kap, dc, name):
+            cn[(kap, dc)] = coefp.tile([P, P, 40], BF16, name=name)
+            nc.sync.dma_start(
+                out=cn[(kap, dc)][:],
+                in_=coef_v[kap * P : (kap + 1) * P, dc * P : (dc + 1) * P, :],
+            )
+
+        def sh_load(n):
+            sh_of[n] = opool.tile([P, 512], BF16, name="sh", bufs=3)
+            for b in range(2):
+                nc.sync.dma_start(out=sh_of[n][b * 64 : (b + 1) * 64, :], in_=shift_v[n * 64 : (n + 1) * 64, :])
+
+        x_sb = coefp.tile([P, 6, 512], BF16, name="late2")
+        w_sb = [coefp.tile([P, 10, 512], BF16, name="late0"), coefp.tile([P, 10, 512], BF16, name="late1")]
+        nc.sync.dma_start(out=x_sb[:, 0:6:3, :], in_=x_v[:, 0:6:3, :])
+        nc.sync.dma_start(out=w_sb[0][:, 0:5, :], in_=w_v[:, 0])
+        nc.sync.dma_start(out=lb[0:20, :], in_=lin_b.rearrange("(t p) -> t p", p=P))
+        nc.sync.dma_start(out=g_row[0:1, :], in_=grid.rearrange("(o g) f -> o (g f)", o=1))
+        for dc in range(1, 4):
+            nc.sync.dma_start(out=w_sb[dc // 2][:, 5 * (dc % 2) : 5 * (dc % 2) + 5, :], in_=w_v[:, dc])
+        nc.sync.dma_start(out=x_sb[:, 1:3, :], in_=x_v[:, 1:3, :])
+        nc.sync.dma_start(out=x_sb[:, 4:6, :], in_=x_v[:, 4:6, :])
+        for n in range(3):
+            sh_load(n)
+        for dc in range(3):
+            for kap in range(3):
+                load_coef(kap, dc, "cn%d_%d" % (kap, dc))
+
+        x32 = x_sb[:].bitcast(F32)
+        w32 = [w_sb[0][:].bitcast(F32), w_sb[1][:].bitcast(F32)]
+
+        def x_words(t):
+            return x32[:, t, :]
+
+        def w_words(beta):
+            return w32[beta // 10][:, beta % 10, :]
+
+        def turn(pool, name, words_a, words_b):
+            tp = pool.tile([P, 2, 2, P], F32, name=name)
             for e in range(2):
-                dc, cc = divmod(2 * t + e, 5)
-                ch = (cc * 4 + dc) * P
+                words = words_a if e == 0 else words_b
+                for u in range(2):
+                    nc.tensor.transpose(tp[:, e, u, :], words[:, u:256:2], ident_f[:])
+            return tp
+
+        def chunk(rows):
+            return ppool.tile([P, rows, 4], BF16, name="pt", align_bytes=64)
+
+        def empty(tp, grouped, lo, on_vector):
+            dst = grouped[:].bitcast(F32)[:, lo : lo + 2 * P, :].rearrange("p (e r) u -> p e r u", e=2)
+            src = tp[:].rearrange("p e u r -> p e r u")
+            if on_vector:
+                nc.vector.tensor_copy(out=dst, in_=src)
+            else:
+                nc.scalar.copy(out=dst, in_=src)
+
+        def quant(grouped, lo, hi, codes, scales, col):
+            nc.vector.quantize_mx(
+                out=codes[:, col : col + hi - lo].bitcast(FP8X4),
+                scales=scales[:, col : col + hi - lo],
+                in_=grouped[:, lo:hi, :].rearrange("p r t -> p (r t)"),
+            )
+
+        def xmm(j, t):
+            c0 = geometry(j)[1]
+            xq_of[(j, t)] = psx.tile([P, 2, 2, P], F32, name="xq")
+            for e in range(2):
+                ch = (2 * t + e) * P
                 for b in range(2):
-                    col = b * 384 + cur["c0"] * 64
+                    col = b * 384 + c0 * 64
                     nc.tensor.matmul_mx(
-                        out=xq_of[t][:, e, b, :],
+                        out=xq_of[(j, t)][:, e, b, :],
                         lhsT=wc[:, ch : ch + P].bitcast(FP8X4),
                         lhsT_scale=ws[:, ch : ch + P],
                         rhs=xc[:, col : col + P].bitcast(FP8X4),
@@ -169,44 +176,34 @@ def tile_ka_attention_heads_mod_pa_kernel(tc, x, lin_w, lin_b, grid, coef, shift
                         stop=True,
                     )
 
-        def x_geometry(j):
-            r_lo = (384 * j) // 5
-            cur["n"] = (384 * j + 383) // 5 + 1 - r_lo
-            cur["c0"] = r_lo // 64
-            cur["a"] = r_lo - 64 * cur["c0"]
-
-        def xev(j, t, first):
-            n = cur["n"]
-            a = cur["a"]
-            if t == 0:
-                xt[j] = xpool.tile([P, 2, 4, 390], F32, name="xt")
-            for e in range(2):
-                dc, cc = divmod(2 * t + e, 5)
-                if cc == 0:
-                    cur["tmp"] = tpool.tile([P, 5, 2, 78], F32, name="tmp")
-                if first and e == 1:
-                    nc.vector.tensor_scalar(
-                        out=cur["tmp"][:, cc, :, 0:n],
-                        in0=xq_of[t][:, e, :, a : a + n],
-                        scalar1=bias_t[:, cc * 4 + dc : cc * 4 + dc + 1],
-                        scalar2=None,
-                        op0=ALU.add,
-                    )
+        def xev_unit(j, beta, on_vector, weave_on_vector):
+            n, c0, a = geometry(j)
+            dc, cc = divmod(beta, 5)
+            if beta == 0:
+                xt[j] = xpool.tile([P, 2, 4, 400], F32, name="xt", align_bytes=64)
+            if cc == 0:
+                cur["tmp"] = tpool.tile([P, 5, 2, 78], F32, name="tmp")
+            src = xq_of[(j, beta // 2)][:, beta % 2, :, a : a + n]
+            dst = cur["tmp"][:, cc, :, 0:n]
+            bias = bias_t[:, cc * 4 + dc : cc * 4 + dc + 1]
+            if on_vector:
+                nc.vector.tensor_scalar(out=dst, in0=src, scalar1=bias, scalar2=None, op0=ALU.add)
+            else:
+                nc.scalar.activation(out=dst, in_=src, func=ACT.Identity, bias=bias, scale=1.0)
+            if cc == 4:
+                dst = xt[j][:, :, dc, 0 : 5 * n].rearrange("p b (r c) -> p b r c", c=5)
+                src = cur["tmp"][:, :, :, 0:n].rearrange("p c b r -> p b r c")
+                if weave_on_vector:
+                    nc.vector.tensor_copy(out=dst, in_=src)
                 else:
-                    nc.scalar.activation(
-                        out=cur["tmp"][:, cc, :, 0:n],
-                        in_=xq_of[t][:, e, :, a : a + n],
-                        func=ACT.Identity,
-                        bias=bias_t[:, cc * 4 + dc : cc * 4 + dc + 1],
-                        scale=1.0,
-                    )
-                if cc == 4:
-                    dst = xt[j][:, :, dc, 0 : 5 * n].rearrange("p b (r c) -> p b r c", c=5)
-                    src = cur["tmp"][:, :, :, 0:n].rearrange("p c b r -> p b r c")
-                    if first:
-                        nc.vector.tensor_copy(out=dst, in_=src)
-                    else:
-                        nc.scalar.copy(out=dst, in_=src)
+                    nc.scalar.copy(out=dst, in_=src)
+
+        def xev_later(j, t):
+            def run():
+                xev_unit(j, 2 * t, False, False)
+                xev_unit(j, 2 * t + 1, False, False)
+
+            return run
 
         def x_slice(s, b):
             j = s // 8
@@ -214,10 +211,9 @@ def tile_ka_attention_heads_mod_pa_kernel(tc, x, lin_w, lin_b, grid, coef, shift
             return xt[j][:, b, :, o : o + 384]
 
         def do_k(s):
-            eng = nc.vector if s == 0 else nc.gpsimd
             for b in range(2):
                 kt_of[(s, b)] = kpool.tile([P, 4, 384], I32, name="kt%d" % b)
-                eng.tensor_scalar(
+                nc.gpsimd.tensor_scalar(
                     out=kt_of[(s, b)][:],
                     in0=x_slice(s, b),
                     scalar1=gsc[:, s : s + 1],
@@ -253,18 +249,13 @@ def tile_ka_attention_heads_mod_pa_kernel(tc, x, lin_w, lin_b, grid, coef, shift
             sel = (q % 4) // 2
             h = q % 2
             if sel == 0:
-                pt[h] = ppool.tile([P, 4, 4, 4, 32], F32, name="pt")
+                pt[h] = ppool.tile([P, 4, 4, 4, 32], F32, name="pt", align_bytes=64)
             nc.vector.tensor_tensor(
                 out=pt[h][:].rearrange("p c i (b s) q -> p b c i s q", b=2)[:, :, :, :, sel, :],
                 in0=s_of[j * 8 + m][:, :, :, kap * P : (kap + 1) * P].rearrange("p b c (i q) -> p b c i q", i=4),
                 in1=ct_of[g][:].rearrange("p c (i q) -> p c i q", i=4).unsqueeze(1).to_broadcast([P, 2, 4, 4, 32]),
                 op=ALU.mult,
             )
-
-        def sh_load(n):
-            sh_of[n] = opool.tile([P, 512], BF16, name="sh", bufs=3)
-            for b in range(2):
-                nc.sync.dma_start(out=sh_of[n][b * 64 : (b + 1) * 64, :], in_=shift_v[n * 64 : (n + 1) * 64, :])
 
         def sh_turn(n):
             cts_of[n] = psc.tile([P, 4, P], BF16, name="ct")
@@ -278,20 +269,23 @@ def tile_ka_attention_heads_mod_pa_kernel(tc, x, lin_w, lin_b, grid, coef, shift
 
             return run
 
+        def open_acc(n, pool, name):
+            acc_of[n] = pool.tile([P, 512], F32, name=name)
+            if plain_shift(n):
+                nc.tensor.matmul(out=acc_of[n][:], lhsT=ident_b[:], rhs=sh_of[n][:], start=True, stop=False)
+            for dc in range(0 if plain_shift(n) else 4):
+                nc.tensor.matmul(
+                    out=acc_of[n][:, dc * P : (dc + 1) * P],
+                    lhsT=sht_of[n][:, dc, :],
+                    rhs=ident_f[:],
+                    is_transpose=True,
+                    start=(dc == 0),
+                    stop=False,
+                )
+
         def do_ta(n, h):
             if h == 0:
-                acc_of[n] = psa.tile([P, 512], F32, name="acc")
-                if plain_shift(n):
-                    nc.tensor.matmul(out=acc_of[n][:], lhsT=ident_b[:], rhs=sh_of[n][:], start=True, stop=False)
-                for dc in range(0 if plain_shift(n) else 4):
-                    nc.tensor.matmul(
-                        out=acc_of[n][:, dc * P : (dc + 1) * P],
-                        lhsT=sht_of[n][:, dc, :],
-                        rhs=ident_f[:],
-                        is_transpose=True,
-                        start=(dc == 0),
-                        stop=False,
-                    )
+                open_acc(n, psa, "acc")
             for dc in range(4):
                 for i in range(4):
                     nc.tensor.matmul(
@@ -308,7 +302,7 @@ def tile_ka_attention_heads_mod_pa_kernel(tc, x, lin_w, lin_b, grid, coef, shift
             rows = slice(n * 64, (n + 1) * 64)
 
             def evac():
-                t["o"] = opool.tile([P, 512], F32, name="o")
+                t["o"] = opool.tile([P, 512], F32, name="o", align_bytes=64)
                 nc.scalar.copy(out=t["o"][:], in_=acc_of[n][:])
                 for b in range(2):
                     nc.sync.dma_start(out=out0_v[b, rows, :], in_=t["o"][b * 64 : (b + 1) * 64, :])
@@ -339,34 +333,216 @@ def tile_ka_attention_heads_mod_pa_kernel(tc, x, lin_w, lin_b, grid, coef, shift
 
             return evac, amax, recip, cast
 
-        def xev_later(j, t):
-            def run():
-                xev(j, t, False)
+        def k_phase(p, eng):
+            for half in range(2):
+                kph[half] = kpool.tile([P, 2, 2, 384], I32, name="kt%d" % half)
+                for mm in range(2):
+                    m = 2 * half + mm
+                    eng.tensor_scalar(
+                        out=kph[half][:, mm],
+                        in0=xt[0][:, :, p, 0:384],
+                        scalar1=gsc[:, m : m + 1],
+                        scalar2=0.0,
+                        op0=ALU.mult,
+                        op1=ALU.add,
+                    )
 
-            return run
+        def r_phase(p, half):
+            if half == 0:
+                sph[p] = spool.tile([P, 2, 4, 384], F32, name="st")
+            for mm in range(2):
+                m = 2 * half + mm
+                nc.vector.scalar_tensor_tensor(
+                    out=sph[p][:, :, m, :],
+                    in0=xt[0][:, :, p, 0:384],
+                    scalar=gsc[:, m : m + 1],
+                    in1=kph[half][:, mm],
+                    op0=ALU.mult,
+                    op1=ALU.subtract,
+                )
 
-        sh_load(0)
-        sh_load(1)
-        x_geometry(0)
-        xmm(0)
-        for t in range(10):
-            if t + 1 < 10:
-                xmm(t + 1)
-            xev(0, t, True)
-        do_k(0)
-        do_r(0)
-        do_k(1)
-        do_r(1)
-        do_k(2)
-        do_ct(0)
-        do_ct(1)
+        def sin_phase(p, half):
+            part = sph[p][:, :, 2 * half : 2 * half + 2, :]
+            nc.scalar.activation(out=part, in_=part, func=ACT.Sin, scale=TWO_PI)
 
-        casts = []
-        evacs = []
-        copies = []
+        def ct_phase(p, n):
+            cth[(p, n)] = psc.tile([P, 4, P], BF16, name="ct")
+            for gg in range(4):
+                m, kap = divmod(4 * n + gg, 3)
+                nc.tensor.transpose(cth[(p, n)][:, gg, :], cn[(kap, p)][:, :, m * 5], ident_b[:])
+
+        def m_phase(p, n):
+            pth[n] = ppool.tile([P, 8, 4, 32], F32, name="pt", align_bytes=64)
+            flat = sph[p][:].rearrange("p b m c -> p b (m c)")
+            for sel in range(2):
+                g0 = 4 * n + 2 * sel
+                nc.vector.tensor_tensor(
+                    out=pth[n][:].rearrange("p e (b s) q -> p b e s q", b=2)[:, :, :, sel, :],
+                    in0=flat[:, :, g0 * P : (g0 + 2) * P].rearrange("p b (e q) -> p b e q", q=32),
+                    in1=cth[(p, n)][:, 2 * sel : 2 * sel + 2, :]
+                    .rearrange("p h (i q) -> p (h i) q", q=32)
+                    .unsqueeze(1)
+                    .to_broadcast([P, 2, 8, 32]),
+                    op=ALU.mult,
+                )
+
+        def ta_phase(p, n):
+            for e in range(8):
+                nc.tensor.matmul(
+                    out=acc_of[n][:, p * P : (p + 1) * P],
+                    lhsT=pth[n][:, e].rearrange("p a q -> p (a q)"),
+                    rhs=ident_f[:],
+                    is_transpose=True,
+                    start=False,
+                    stop=(p == 3 and e == 7),
+                )
+
+        tp_x = turn(psc, "ct", x_words(0), x_words(3))
+        tp = {}
+        for i in range(3):
+            tp[i] = turn(psc, "ct", w_words(2 * i), w_words(2 * i + 1))
+        gxa = chunk(256)
+        empty(tp_x, gxa, 0, True)
+        c0 = chunk(512)
+        empty(tp[0], c0, 0, False)
+        empty(tp[1], c0, 256, True)
+        c1 = chunk(256)
+        empty(tp[2], c1, 0, False)
+        tb = psc.tile([P, P], BF16, name="ct")
+        nc.tensor.transpose(tb[:], lb[:], ident_b[:])
+        nc.vector.tensor_copy(out=bias_t[:], in_=tb[:, 0:20])
+        gp = psc.tile([P, 40], F32, name="ct")
+        nc.tensor.matmul(out=gp[:], lhsT=first_row[:], rhs=g_row[:], start=True, stop=True)
+        nc.vector.tensor_scalar(out=gsc[:], in0=gp[:], scalar1=1.0 / TWO_PI, scalar2=None, op0=ALU.mult)
+        quant(gxa, 0, 128, xc, xs, 0)
+        quant(gxa, 128, 256, xc, xs, 384)
+        quant(c0, 0, 512, wc, ws, 0)
+        quant(c1, 0, 256, wc, ws, 512)
+        tp[3] = turn(psc, "ct", w_words(6), w_words(7))
+        tp[4] = turn(psc, "ct", w_words(8), w_words(9))
+        xmm(0, 0)
+        xmm(0, 1)
+        c2 = chunk(512)
+        empty(tp[3], c2, 0, False)
+        empty(tp[4], c2, 256, True)
+        xev_unit(0, 0, False, True)
+        xev_unit(0, 1, True, True)
+        xev_unit(0, 2, False, True)
+        xev_unit(0, 3, True, True)
+        xmm(0, 2)
+        quant(c2, 0, 512, wc, ws, 768)
+        tp[5] = turn(psc, "ct", w_words(10), w_words(11))
+        tp[6] = turn(psc, "ct", w_words(12), w_words(13))
+        xev_unit(0, 4, False, True)
+        xev_unit(0, 5, False, True)
+        xmm(0, 3)
+        xmm(0, 4)
+        k_phase(0, nc.vector)
+        for beta in range(6, 10):
+            xev_unit(0, beta, False, False)
+        r_phase(0, 0)
+        c3 = chunk(512)
+        empty(tp[5], c3, 0, False)
+        empty(tp[6], c3, 256, False)
+        r_phase(0, 1)
+        for i in range(7, 10):
+            tp[i] = turn(psc, "ct", w_words(2 * i), w_words(2 * i + 1))
+        sin_phase(0, 0)
+        c4 = chunk(512)
+        empty(tp[7], c4, 0, False)
+        empty(tp[8], c4, 256, False)
+        quant(c3, 0, 512, wc, ws, 1280)
+        quant(c4, 0, 512, wc, ws, 1792)
+        sin_phase(0, 1)
+        xmm(0, 5)
+        xmm(0, 6)
+        k_phase(1, nc.vector)
+        for beta in range(10, 14):
+            xev_unit(0, beta, False, False)
+        xmm(0, 7)
+        xev_unit(0, 14, False, False)
+        xev_unit(0, 15, False, False)
+        r_phase(1, 0)
+        r_phase(1, 1)
+        c5 = chunk(256)
+        empty(tp[9], c5, 0, False)
+        for n in range(3):
+            ct_phase(0, n)
+        for n in (1, 2):
+            sh_turn(n)
+            sh_copy(n)()
+        open_acc(0, psa, "acc")
+        open_acc(1, psa, "acc")
+        open_acc(2, psc, "ct")
+        sin_phase(1, 0)
+        sin_phase(1, 1)
+        quant(c5, 0, 256, wc, ws, 2304)
+        xmm(0, 8)
+        xev_unit(0, 16, False, False)
+        xev_unit(0, 17, False, False)
+        xmm(0, 9)
+        xev_unit(0, 18, False, False)
+        xev_unit(0, 19, False, False)
+        tp_y = turn(psx, "xq", x_words(1), x_words(2))
+        tp_z = turn(psx, "xq", x_words(4), x_words(5))
+        for kap in range(3):
+            load_coef(kap, 3, "late%d" % kap)
+        sh_load(3)
+        sh_load(4)
+        gxb = opool.tile([P, 256, 4], BF16, name="o", align_bytes=64)
+        empty(tp_y, gxb, 0, False)
+        gxc = opool.tile([P, 256, 4], BF16, name="o", align_bytes=64)
+        empty(tp_z, gxc, 0, False)
+
+        chains = {}
         xevs = []
-        dve_small = []
-        for s in range(40):
+        for p in range(HEAD):
+            if p < 3:
+                for fn in xevs:
+                    fn()
+                xevs = []
+            if p < 2:
+                k_phase(p + 2, nc.gpsimd)
+            else:
+                do_k(p + 2)
+            for n in range(3):
+                m_phase(p, n)
+                ta_phase(p, n)
+                if p < 3:
+                    ct_phase(p + 1, n)
+                else:
+                    chains[n] = out_chain(n)
+                    if n < 2:
+                        do_ct(3 * HEAD + n)
+                    if n >= 1:
+                        chains[n - 1][0]()
+            if p < 2:
+                r_phase(p + 2, 0)
+                sin_phase(p + 2, 0)
+                r_phase(p + 2, 1)
+                sin_phase(p + 2, 1)
+            elif p == 2:
+                do_r(HEAD)
+            else:
+                chains[0][1]()
+                chains[0][2]()
+                for fn in xevs:
+                    fn()
+                xevs = []
+            if p == 0:
+                quant(gxb, 0, 256, xc, xs, 128)
+                quant(gxc, 0, 256, xc, xs, 512)
+            if p >= 1:
+                for t in (2 * p - 2, 2 * p - 1):
+                    xmm(1, t)
+                    xevs.extend([xev_later(1, t)])
+
+        casts = [chains[0][3]]
+        late_casts = [chains[1][3]]
+        evacs = [chains[2]]
+        copies = []
+        dve_small = [chains[1][1], chains[1][2]]
+        for s in range(HEAD, 40):
             j, m = divmod(s, 8)
             for fn in casts:
                 fn()
@@ -374,7 +550,8 @@ def tile_ka_attention_heads_mod_pa_kernel(tc, x, lin_w, lin_b, grid, coef, shift
             for fns in evacs:
                 fns[0]()
                 new_small.extend([fns[1], fns[2]])
-            cast_next = [fns[3] for fns in evacs]
+            cast_next = late_casts + [fns[3] for fns in evacs]
+            late_casts = []
             for fn in copies + xevs:
                 fn()
             casts = cast_next
@@ -390,7 +567,7 @@ def tile_ka_attention_heads_mod_pa_kernel(tc, x, lin_w, lin_b, grid, coef, shift
                 g = 3 * s + kap
                 if g + 2 < 120:
                     do_ct(g + 2)
-                if g >= 1 and (g - 1) % 4 >= 2:
+                if (g - 1) % 4 >= 2 and (g - 1) // 4 >= 3:
                     do_ta((g - 1) // 4, (g - 1) % 2)
                     if (g - 1) % 4 == 3:
                         evacs.extend([out_chain((g - 1) // 4)])
@@ -401,14 +578,14 @@ def tile_ka_attention_heads_mod_pa_kernel(tc, x, lin_w, lin_b, grid, coef, shift
                     if g // 4 + 2 < 30:
                         sh_load(g // 4 + 2)
                 do_m(g)
-                if dve_small:
-                    dve_small[0]()
-                    dve_small = dve_small[1:]
-            if j < 4 and m <= 4:
-                if m == 0:
-                    x_geometry(j + 1)
-                for t in (2 * m, 2 * m + 1):
-                    xmm(t)
+                for rep in range(2 if len(dve_small) >= 3 else 1):
+                    if dve_small:
+                        dve_small[0]()
+                        dve_small = dve_small[1:]
+            lag = 1 if j == 0 else 0
+            if j < 4 and m - lag <= 4:
+                for t in (2 * (m - lag), 2 * (m - lag) + 1):
+                    xmm(j + 1, t)
                     xevs.extend([xev_later(j + 1, t)])
         do_ta(29, 1)
         last = out_chain(29)

@@ -211,16 +211,19 @@ def tile_ka_attention_heads_mod_pa_kernel(tc, x, lin_w, lin_b, grid, coef, shift
             return xt[j][:, b, :, o : o + 384]
 
         def do_k(s):
+            j = s // 8
+            o = 384 * j - 5 * ((384 * j) // 5)
+            both = kpool.tile([P, 2, 4, 384], I32, name="kt")
             for b in range(2):
-                kt_of[(s, b)] = kpool.tile([P, 4, 384], I32, name="kt%d" % b)
-                nc.gpsimd.tensor_scalar(
-                    out=kt_of[(s, b)][:],
-                    in0=x_slice(s, b),
-                    scalar1=gsc[:, s : s + 1],
-                    scalar2=0.0,
-                    op0=ALU.mult,
-                    op1=ALU.add,
-                )
+                kt_of[(s, b)] = both[:, b]
+            nc.gpsimd.tensor_scalar(
+                out=both[:],
+                in0=xt[j][:, :, :, o : o + 384],
+                scalar1=gsc[:, s : s + 1],
+                scalar2=0.0,
+                op0=ALU.mult,
+                op1=ALU.add,
+            )
 
         def do_r(s):
             s_of[s] = spool.tile([P, 2, 4, 384], F32, name="st")
@@ -229,7 +232,7 @@ def tile_ka_attention_heads_mod_pa_kernel(tc, x, lin_w, lin_b, grid, coef, shift
                     out=s_of[s][:, b],
                     in0=x_slice(s, b),
                     scalar=gsc[:, s : s + 1],
-                    in1=kt_of[(s, b)][:],
+                    in1=kt_of[(s, b)],
                     op0=ALU.mult,
                     op1=ALU.subtract,
                 )
@@ -334,8 +337,9 @@ def tile_ka_attention_heads_mod_pa_kernel(tc, x, lin_w, lin_b, grid, coef, shift
             return evac, amax, recip, cast
 
         def k_phase(p, eng):
+            whole = kpool.tile([P, 2, 2, 2, 384], I32, name="kt")
             for half in range(2):
-                kph[half] = kpool.tile([P, 2, 2, 384], I32, name="kt%d" % half)
+                kph[half] = whole[:, half]
                 for mm in range(2):
                     m = 2 * half + mm
                     eng.tensor_scalar(

@@ -214,8 +214,8 @@ def tile_ka_attention_heads_mod_pa_kernel(tc, x, lin_w, lin_b, grid, coef, shift
             j = s // 8
             o = 384 * j - 5 * ((384 * j) // 5)
             both = kpool.tile([P, 2, 4, 384], I32, name="kt")
-            for b in range(2):
-                kt_of[(s, b)] = both[:, b]
+            kt_of[s] = both[:]
+            kt_of[(s, 0)] = True
             nc.gpsimd.tensor_scalar(
                 out=both[:],
                 in0=xt[j][:, :, :, o : o + 384],
@@ -227,15 +227,16 @@ def tile_ka_attention_heads_mod_pa_kernel(tc, x, lin_w, lin_b, grid, coef, shift
 
         def do_r(s):
             s_of[s] = spool.tile([P, 2, 4, 384], F32, name="st")
-            for b in range(2):
-                nc.vector.scalar_tensor_tensor(
-                    out=s_of[s][:, b],
-                    in0=x_slice(s, b),
-                    scalar=gsc[:, s : s + 1],
-                    in1=kt_of[(s, b)],
-                    op0=ALU.mult,
-                    op1=ALU.subtract,
-                )
+            j = s // 8
+            o = 384 * j - 5 * ((384 * j) // 5)
+            nc.vector.scalar_tensor_tensor(
+                out=s_of[s][:],
+                in0=xt[j][:, :, :, o : o + 384],
+                scalar=gsc[:, s : s + 1],
+                in1=kt_of[s],
+                op0=ALU.mult,
+                op1=ALU.subtract,
+            )
             for b in range(2):
                 nc.scalar.activation(out=s_of[s][:, b], in_=s_of[s][:, b], func=ACT.Sin, scale=TWO_PI)
 
@@ -536,10 +537,9 @@ def tile_ka_attention_heads_mod_pa_kernel(tc, x, lin_w, lin_b, grid, coef, shift
             if p == 0:
                 quant(gxb, 0, 256, xc, xs, 128)
                 quant(gxc, 0, 256, xc, xs, 512)
-            if p >= 1:
-                for t in (2 * p - 2, 2 * p - 1):
-                    xmm(1, t)
-                    xevs.extend([xev_later(1, t)])
+            for t in (2 * p, 2 * p + 1):
+                xmm(1, t)
+                xevs.extend([xev_later(1, t)])
 
         casts = [chains[0][3]]
         late_casts = [chains[1][3]]
@@ -586,9 +586,8 @@ def tile_ka_attention_heads_mod_pa_kernel(tc, x, lin_w, lin_b, grid, coef, shift
                     if dve_small:
                         dve_small[0]()
                         dve_small = dve_small[1:]
-            lag = 1 if j == 0 else 0
-            if j < 4 and m - lag <= 4:
-                for t in (2 * (m - lag), 2 * (m - lag) + 1):
+            if j < 4 and m <= 4:
+                for t in (2 * m, 2 * m + 1):
                     xmm(j + 1, t)
                     xevs.extend([xev_later(j + 1, t)])
         do_ta(29, 1)

@@ -105,8 +105,11 @@ def tile_ka_attention_heads_mod_pa_kernel(tc, x, lin_w, lin_b, grid, coef, shift
 
         def sh_load(n):
             sh_of[n] = opool.tile([P, 512], BF16, name="sh", bufs=3)
-            for b in range(2):
-                nc.sync.dma_start(out=sh_of[n][b * 64 : (b + 1) * 64, :], in_=shift_v[n * 64 : (n + 1) * 64, :])
+            if plain_shift(n):
+                for b in range(2):
+                    nc.sync.dma_start(out=sh_of[n][b * 64 : (b + 1) * 64, :], in_=shift_v[n * 64 : (n + 1) * 64, :])
+            else:
+                nc.sync.dma_start(out=sh_of[n][:], in_=shift_v[n * 64 : (n + 2) * 64, :])
 
         x_sb = coefp.tile([P, 6, 512], BF16, name="late2")
         w_sb = [coefp.tile([P, 10, 512], BF16, name="late0"), coefp.tile([P, 10, 512], BF16, name="late1")]
@@ -118,7 +121,7 @@ def tile_ka_attention_heads_mod_pa_kernel(tc, x, lin_w, lin_b, grid, coef, shift
             nc.sync.dma_start(out=w_sb[dc // 2][:, 5 * (dc % 2) : 5 * (dc % 2) + 5, :], in_=w_v[:, dc])
         nc.sync.dma_start(out=x_sb[:, 1:3, :], in_=x_v[:, 1:3, :])
         nc.sync.dma_start(out=x_sb[:, 4:6, :], in_=x_v[:, 4:6, :])
-        for n in range(3):
+        for n in range(2):
             sh_load(n)
         for dc in range(3):
             for kap in range(3):
@@ -268,8 +271,12 @@ def tile_ka_attention_heads_mod_pa_kernel(tc, x, lin_w, lin_b, grid, coef, shift
 
         def sh_copy(n):
             def run():
-                sht_of[n] = opool.tile([P, 4, P], F32, name="sht")
-                nc.scalar.copy(out=sht_of[n][:], in_=cts_of[n][:])
+                for k in range(2):
+                    sht_of[n + k] = opool.tile([P, 4, P], F32, name="sht")
+                    nc.scalar.copy(
+                        out=sht_of[n + k][:].rearrange("p c (b r) -> p c b r", b=2),
+                        in_=cts_of[n][:, :, k * 64 : (k + 1) * 64].unsqueeze(2).to_broadcast([P, 4, 2, 64]),
+                    )
 
             return run
 
@@ -473,9 +480,8 @@ def tile_ka_attention_heads_mod_pa_kernel(tc, x, lin_w, lin_b, grid, coef, shift
         empty(tp[9], c5, 0, False)
         for n in range(3):
             ct_phase(0, n)
-        for n in (1, 2):
-            sh_turn(n)
-            sh_copy(n)()
+        sh_turn(1)
+        sh_copy(1)()
         open_acc(0, psa, "acc")
         open_acc(1, psa, "acc")
         open_acc(2, psc, "ct")
@@ -575,12 +581,12 @@ def tile_ka_attention_heads_mod_pa_kernel(tc, x, lin_w, lin_b, grid, coef, shift
                     do_ta((g - 1) // 4, (g - 1) % 2)
                     if (g - 1) % 4 == 3:
                         evacs.extend([out_chain((g - 1) // 4)])
-                if g % 4 == 0 and g // 4 + 1 < 30:
-                    if not plain_shift(g // 4 + 1):
-                        sh_turn(g // 4 + 1)
-                        copies.extend([sh_copy(g // 4 + 1)])
-                    if g // 4 + 2 < 30:
-                        sh_load(g // 4 + 2)
+                if g % 12 == 0:
+                    sh_turn(g // 4 + 1)
+                    copies.extend([sh_copy(g // 4 + 1)])
+                    if g // 4 + 3 < 30:
+                        sh_load(g // 4 + 3)
+                        sh_load(g // 4 + 4)
                 do_m(g)
                 for rep in range(2 if len(dve_small) >= 3 else 1):
                     if dve_small:

@@ -269,14 +269,13 @@ def tile_ka_attention_heads_mod_pa_kernel(tc, x, lin_w, lin_b, grid, coef, shift
             for dc in range(4):
                 nc.tensor.transpose(cts_of[n][:, dc, :], sh_of[n][:, dc * P : (dc + 1) * P], ident_b[:])
 
-        def sh_copy(n):
+        def sh_copy(n, k):
             def run():
-                for k in range(2):
-                    sht_of[n + k] = opool.tile([P, 4, P], F32, name="sht")
-                    nc.scalar.copy(
-                        out=sht_of[n + k][:].rearrange("p c (b r) -> p c b r", b=2),
-                        in_=cts_of[n][:, :, k * 64 : (k + 1) * 64].unsqueeze(2).to_broadcast([P, 4, 2, 64]),
-                    )
+                sht_of[n + k] = opool.tile([P, 4, P], F32, name="sht")
+                nc.scalar.copy(
+                    out=sht_of[n + k][:].rearrange("p c (b r) -> p c b r", b=2),
+                    in_=cts_of[n][:, :, k * 64 : (k + 1) * 64].unsqueeze(2).to_broadcast([P, 4, 2, 64]),
+                )
 
             return run
 
@@ -481,7 +480,8 @@ def tile_ka_attention_heads_mod_pa_kernel(tc, x, lin_w, lin_b, grid, coef, shift
         for n in range(3):
             ct_phase(0, n)
         sh_turn(1)
-        sh_copy(1)()
+        sh_copy(1, 0)()
+        sh_copy(1, 1)()
         open_acc(0, psa, "acc")
         open_acc(1, psa, "acc")
         open_acc(2, psc, "ct")
@@ -551,6 +551,7 @@ def tile_ka_attention_heads_mod_pa_kernel(tc, x, lin_w, lin_b, grid, coef, shift
         late_casts = [chains[1][3]]
         evacs = [chains[2]]
         copies = []
+        copies_later = []
         dve_small = [chains[1][1], chains[1][2]]
         for s in range(HEAD, 40):
             j, m = divmod(s, 8)
@@ -566,7 +567,8 @@ def tile_ka_attention_heads_mod_pa_kernel(tc, x, lin_w, lin_b, grid, coef, shift
                 fn()
             casts = cast_next
             evacs = []
-            copies = []
+            copies = copies_later
+            copies_later = []
             xevs = []
             dve_small.extend(new_small)
             if s + 1 < 40 and s + 1 not in s_of:
@@ -583,7 +585,8 @@ def tile_ka_attention_heads_mod_pa_kernel(tc, x, lin_w, lin_b, grid, coef, shift
                         evacs.extend([out_chain((g - 1) // 4)])
                 if g % 12 == 0:
                     sh_turn(g // 4 + 1)
-                    copies.extend([sh_copy(g // 4 + 1)])
+                    copies.extend([sh_copy(g // 4 + 1, 0)])
+                    copies_later.extend([sh_copy(g // 4 + 1, 1)])
                     if g // 4 + 3 < 30:
                         sh_load(g // 4 + 3)
                         sh_load(g // 4 + 4)

@@ -240,8 +240,7 @@ def tile_ka_attention_heads_mod_pa_kernel(tc, x, lin_w, lin_b, grid, coef, shift
                 op0=ALU.mult,
                 op1=ALU.subtract,
             )
-            for b in range(2):
-                nc.scalar.activation(out=s_of[s][:, b], in_=s_of[s][:, b], func=ACT.Sin, scale=TWO_PI)
+            nc.scalar.activation(out=s_of[s][:], in_=s_of[s][:], func=ACT.Sin, scale=TWO_PI)
 
         def do_ct(g):
             j, q = divmod(g, 24)

@@ -39,8 +39,7 @@ def tile_ka_attention_heads_mod_pa_kernel(tc, x, lin_w, lin_b, grid, coef, shift
         coefp = ctx.enter_context(tc.tile_pool(name="coefp", bufs=1))
         xpool = ctx.enter_context(tc.tile_pool(name="xpool", bufs=2))
         tpool = ctx.enter_context(tc.tile_pool(name="tpool", bufs=1))
-        kpool = ctx.enter_context(tc.tile_pool(name="kpool", bufs=1))
-        spool = ctx.enter_context(tc.tile_pool(name="spool", bufs=2))
+        spool = ctx.enter_context(tc.tile_pool(name="spool", bufs=3))
         ppool = ctx.enter_context(tc.tile_pool(name="ppool", bufs=3))
         opool = ctx.enter_context(tc.tile_pool(name="opool", bufs=2))
         psa = ctx.enter_context(tc.psum_pool(name="psa", bufs=2))
@@ -83,6 +82,7 @@ def tile_ka_attention_heads_mod_pa_kernel(tc, x, lin_w, lin_b, grid, coef, shift
         xt = {}
         xq_of = {}
         kt_of = {}
+        r_done = {}
         s_of = {}
         ct_of = {}
         pt = {}
@@ -216,11 +216,11 @@ def tile_ka_attention_heads_mod_pa_kernel(tc, x, lin_w, lin_b, grid, coef, shift
         def do_k(s):
             j = s // 8
             o = 384 * j - 5 * ((384 * j) // 5)
-            both = kpool.tile([P, 2, 4, 384], I32, name="kt")
-            kt_of[s] = both[:]
+            s_of[s] = spool.tile([P, 2, 4, 384], F32, name="st")
+            kt_of[s] = s_of[s][:].bitcast(I32)
             kt_of[(s, 0)] = True
             nc.gpsimd.tensor_scalar(
-                out=both[:],
+                out=kt_of[s],
                 in0=xt[j][:, :, :, o : o + 384],
                 scalar1=gsc[:, s : s + 1],
                 scalar2=0.0,
@@ -229,7 +229,7 @@ def tile_ka_attention_heads_mod_pa_kernel(tc, x, lin_w, lin_b, grid, coef, shift
             )
 
         def do_r(s):
-            s_of[s] = spool.tile([P, 2, 4, 384], F32, name="st")
+            r_done[s] = True
             j = s // 8
             o = 384 * j - 5 * ((384 * j) // 5)
             nc.vector.scalar_tensor_tensor(
@@ -343,13 +343,13 @@ def tile_ka_attention_heads_mod_pa_kernel(tc, x, lin_w, lin_b, grid, coef, shift
             return evac, amax, recip, cast
 
         def k_phase(p, eng):
-            whole = kpool.tile([P, 2, 2, 2, 384], I32, name="kt")
+            sph[p] = spool.tile([P, 2, 4, 384], F32, name="st")
+            kph[p] = sph[p][:].bitcast(I32)
             for half in range(2):
-                kph[half] = whole[:, half]
                 for mm in range(2):
                     m = 2 * half + mm
                     eng.tensor_scalar(
-                        out=kph[half][:, mm],
+                        out=kph[p][:, :, m, :],
                         in0=xt[0][:, :, p, 0:384],
                         scalar1=gsc[:, m : m + 1],
                         scalar2=0.0,
@@ -358,15 +358,13 @@ def tile_ka_attention_heads_mod_pa_kernel(tc, x, lin_w, lin_b, grid, coef, shift
                     )
 
         def r_phase(p, half):
-            if half == 0:
-                sph[p] = spool.tile([P, 2, 4, 384], F32, name="st")
             for mm in range(2):
                 m = 2 * half + mm
                 nc.vector.scalar_tensor_tensor(
                     out=sph[p][:, :, m, :],
                     in0=xt[0][:, :, p, 0:384],
                     scalar=gsc[:, m : m + 1],
-                    in1=kph[half][:, mm],
+                    in1=kph[p][:, :, m, :],
                     op0=ALU.mult,
                     op1=ALU.subtract,
                 )
@@ -513,7 +511,7 @@ def tile_ka_attention_heads_mod_pa_kernel(tc, x, lin_w, lin_b, grid, coef, shift
                 xevs = []
             if p < 2:
                 k_phase(p + 2, nc.gpsimd)
-            else:
+            elif p == 2:
                 do_k(p + 2)
             for n in range(3):
                 m_phase(p, n)
@@ -532,7 +530,9 @@ def tile_ka_attention_heads_mod_pa_kernel(tc, x, lin_w, lin_b, grid, coef, shift
                 r_phase(p + 2, 1)
                 sin_phase(p + 2, 1)
             elif p == 2:
+                do_k(HEAD + 1)
                 do_r(HEAD)
+                do_r(HEAD + 1)
             else:
                 chains[0][1]()
                 chains[0][2]()
@@ -570,7 +570,7 @@ def tile_ka_attention_heads_mod_pa_kernel(tc, x, lin_w, lin_b, grid, coef, shift
             copies_later = []
             xevs = []
             dve_small.extend(new_small)
-            if s + 1 < 40 and s + 1 not in s_of:
+            if s + 1 < 40 and s + 1 not in r_done:
                 do_r(s + 1)
             if s + 2 < 40 and (s + 2, 0) not in kt_of:
                 do_k(s + 2)
@@ -590,10 +590,10 @@ def tile_ka_attention_heads_mod_pa_kernel(tc, x, lin_w, lin_b, grid, coef, shift
                         sh_load(g // 4 + 3)
                         sh_load(g // 4 + 4)
                 do_m(g)
-                for rep in range(2 if len(dve_small) >= 3 else 1):
-                    if dve_small:
-                        dve_small[0]()
-                        dve_small = dve_small[1:]
+                take = 0 if kap == 2 else ((len(dve_small) + 1) // 2 if kap == 0 else len(dve_small))
+                for fn in dve_small[:take]:
+                    fn()
+                dve_small = dve_small[take:]
             if j < 4 and m <= 4:
                 for t in (2 * m, 2 * m + 1):
                     xmm(j + 1, t)

@@ -256,12 +256,19 @@ def tile_ka_attention_heads_mod_pa_kernel(tc, x, lin_w, lin_b, grid, coef, shift
             h = q % 2
             if sel == 0:
                 pt[h] = ppool.tile([P, 4, 4, 4, 32], F32, name="pt", align_bytes=64)
-            nc.vector.tensor_tensor(
-                out=pt[h][:].rearrange("p c i (b s) q -> p b c i s q", b=2)[:, :, :, :, sel, :],
-                in0=s_of[j * 8 + m][:, :, :, kap * P : (kap + 1) * P].rearrange("p b c (i q) -> p b c i q", i=4),
-                in1=ct_of[g][:].rearrange("p c (i q) -> p c i q", i=4).unsqueeze(1).to_broadcast([P, 2, 4, 4, 32]),
-                op=ALU.mult,
-            )
+            width = 1 if g == 119 else 4
+            for c in range(0, 4, width):
+                nc.vector.tensor_tensor(
+                    out=pt[h][:].rearrange("p c i (b s) q -> p b c i s q", b=2)[:, :, c : c + width, :, sel, :],
+                    in0=s_of[j * 8 + m][:, :, c : c + width, kap * P : (kap + 1) * P].rearrange(
+                        "p b c (i q) -> p b c i q", i=4
+                    ),
+                    in1=ct_of[g][:, c : c + width, :]
+                    .rearrange("p c (i q) -> p c i q", i=4)
+                    .unsqueeze(1)
+                    .to_broadcast([P, 2, width, 4, 32]),
+                    op=ALU.mult,
+                )
 
         def sh_turn(n):
             cts_of[n] = psc.tile([P, 4, P], BF16, name="ct")
@@ -378,6 +385,16 @@ def tile_ka_attention_heads_mod_pa_kernel(tc, x, lin_w, lin_b, grid, coef, shift
             for gg in range(4):
                 m, kap = divmod(4 * n + gg, 3)
                 nc.tensor.transpose(cth[(p, n)][:, gg, :], cn[(kap, p)][:, :, m * 5], ident_b[:])
+
+        def ct_last_phase(p):
+            for n in range(3):
+                cth[(p, n)] = psc.tile([P, 4, P], BF16, name="ct")
+            for last_group in (False, True):
+                for n in range(3):
+                    for gg in range(4):
+                        m, kap = divmod(4 * n + gg, 3)
+                        if (kap == 2) == last_group:
+                            nc.tensor.transpose(cth[(p, n)][:, gg, :], cn[(kap, p)][:, :, m * 5], ident_b[:])
 
         def m_phase(p, n):
             pth[n] = ppool.tile([P, 8, 4, 32], F32, name="pt", align_bytes=64)
@@ -516,9 +533,9 @@ def tile_ka_attention_heads_mod_pa_kernel(tc, x, lin_w, lin_b, grid, coef, shift
             for n in range(3):
                 m_phase(p, n)
                 ta_phase(p, n)
-                if p < 3:
+                if p < 2:
                     ct_phase(p + 1, n)
-                else:
+                elif p == 3:
                     chains[n] = out_chain(n)
                     if n < 2:
                         do_ct(3 * HEAD + n)
@@ -545,6 +562,8 @@ def tile_ka_attention_heads_mod_pa_kernel(tc, x, lin_w, lin_b, grid, coef, shift
             for t in (2 * p, 2 * p + 1):
                 xmm(1, t)
                 xevs.extend([xev_later(1, t)])
+            if p == 2:
+                ct_last_phase(3)
 
         casts = [chains[0][3]]
         late_casts = [chains[1][3]]

@@ -593,7 +593,20 @@ def tile_ka_attention_heads_mod_pa_kernel(tc, x, lin_w, lin_b, grid, coef, shift
                 do_r(s + 1)
             if s + 2 < 40 and (s + 2, 0) not in kt_of:
                 do_k(s + 2)
-            for kap in range(3):
+            if s == 39:
+                do_ct(119)
+                do_m(118)
+                take = (len(dve_small) + 1) // 2
+                for fn in dve_small[:take]:
+                    fn()
+                dve_small = dve_small[take:]
+                do_ta(29, 0)
+                do_m(117)
+                for fn in dve_small:
+                    fn()
+                dve_small = []
+                do_m(119)
+            for kap in range(3 if s < 39 else 0):
                 g = 3 * s + kap
                 if g + 2 < 120:
                     do_ct(g + 2)

@@ -245,9 +245,9 @@ def tile_ka_attention_heads_mod_pa_kernel(tc, x, lin_w, lin_b, grid, coef, shift
         def do_ct(g):
             j, q = divmod(g, 24)
             m, kap = divmod(q, 3)
-            ct_of[g] = psc.tile([P, 4, P], BF16, name="ct")
+            ct_of[g] = psc.tile([P, 4, P], F32, name="ct")
             for dc in range(4):
-                nc.tensor.transpose(ct_of[g][:, dc, :], cn[(kap, dc)][:, :, m * 5 + j], ident_b[:])
+                nc.tensor.transpose(ct_of[g][:, dc, :], cn[(kap, dc)][:].bitcast(F32)[:, :, (m * 5 + j) // 2], ident_f[:])
 
         def do_m(g):
             j, q = divmod(g, 24)
@@ -263,8 +263,9 @@ def tile_ka_attention_heads_mod_pa_kernel(tc, x, lin_w, lin_b, grid, coef, shift
                     in0=s_of[j * 8 + m][:, :, c : c + width, kap * P : (kap + 1) * P].rearrange(
                         "p b c (i q) -> p b c i q", i=4
                     ),
-                    in1=ct_of[g][:, c : c + width, :]
-                    .rearrange("p c (i q) -> p c i q", i=4)
+                    in1=ct_of[g][:]
+                    .bitcast(BF16)[:, c : c + width, :]
+                    .rearrange("p c (i q t) -> p c i q t", i=4, t=2)[:, :, :, :, (m * 5 + j) % 2]
                     .unsqueeze(1)
                     .to_broadcast([P, 2, width, 4, 32]),
                     op=ALU.mult,

@@ -566,6 +566,10 @@ def tile_ka_attention_heads_mod_pa_kernel(tc, x, lin_w, lin_b, grid, coef, shift
             if p == 2:
                 ct_last_phase(3)
 
+        x_units = {HEAD: [(1, 8), (1, 9)]}
+        for grp in range(2, 5):
+            for t in range(10):
+                x_units.setdefault(8 * grp - 10 + (7 * t) // 10, []).extend([(grp, t)])
         casts = [chains[0][3]]
         late_casts = [chains[1][3]]
         evacs = [chains[2]]
@@ -627,10 +631,9 @@ def tile_ka_attention_heads_mod_pa_kernel(tc, x, lin_w, lin_b, grid, coef, shift
                 for fn in dve_small[:take]:
                     fn()
                 dve_small = dve_small[take:]
-            if j < 4 and m <= 4:
-                for t in (2 * m, 2 * m + 1):
-                    xmm(j + 1, t)
-                    xevs.extend([xev_later(j + 1, t)])
+            for grp, t in x_units.get(s, []):
+                xmm(grp, t)
+                xevs.extend([xev_later(grp, t)])
         do_ta(29, 1)
         last = out_chain(29)
         for fn in dve_small:

@@ -382,35 +382,40 @@ def tile_ka_attention_heads_mod_pa_kernel(tc, x, lin_w, lin_b, grid, coef, shift
             nc.scalar.activation(out=part, in_=part, func=ACT.Sin, scale=TWO_PI)
 
         def ct_phase(p, n):
-            cth[(p, n)] = psc.tile([P, 4, P], BF16, name="ct")
+            cth[(p, n)] = psc.tile([P, 4, P], F32, name="ct")
             for gg in range(4):
                 m, kap = divmod(4 * n + gg, 3)
-                nc.tensor.transpose(cth[(p, n)][:, gg, :], cn[(kap, p)][:, :, m * 5], ident_b[:])
+                nc.tensor.transpose(cth[(p, n)][:, gg, :], cn[(kap, p)][:].bitcast(F32)[:, :, (m * 5) // 2], ident_f[:])
 
         def ct_last_phase(p):
             for n in range(3):
-                cth[(p, n)] = psc.tile([P, 4, P], BF16, name="ct")
+                cth[(p, n)] = psc.tile([P, 4, P], F32, name="ct")
             for last_group in (False, True):
                 for n in range(3):
                     for gg in range(4):
                         m, kap = divmod(4 * n + gg, 3)
                         if (kap == 2) == last_group:
-                            nc.tensor.transpose(cth[(p, n)][:, gg, :], cn[(kap, p)][:, :, m * 5], ident_b[:])
+                            nc.tensor.transpose(
+                                cth[(p, n)][:, gg, :], cn[(kap, p)][:].bitcast(F32)[:, :, (m * 5) // 2], ident_f[:]
+                            )
 
         def m_phase(p, n):
             pth[n] = ppool.tile([P, 8, 4, 32], F32, name="pt", align_bytes=64)
             flat = sph[p][:].rearrange("p b m c -> p b (m c)")
+            halves = cth[(p, n)][:].bitcast(BF16).rearrange("p h (i q t) -> p h i q t", q=32, t=2)
             for sel in range(2):
                 g0 = 4 * n + 2 * sel
-                nc.vector.tensor_tensor(
-                    out=pth[n][:].rearrange("p e (b s) q -> p b e s q", b=2)[:, :, :, sel, :],
-                    in0=flat[:, :, g0 * P : (g0 + 2) * P].rearrange("p b (e q) -> p b e q", q=32),
-                    in1=cth[(p, n)][:, 2 * sel : 2 * sel + 2, :]
-                    .rearrange("p h (i q) -> p (h i) q", q=32)
-                    .unsqueeze(1)
-                    .to_broadcast([P, 2, 8, 32]),
-                    op=ALU.mult,
-                )
+                width = 2 if (g0 // 3) % 2 == ((g0 + 1) // 3) % 2 else 1
+                for h in range(0, 2, width):
+                    nc.vector.tensor_tensor(
+                        out=pth[n][:].rearrange("p e (b s) q -> p b e s q", b=2)[:, :, 4 * h : 4 * (h + width), sel, :],
+                        in0=flat[:, :, (g0 + h) * P : (g0 + h + width) * P].rearrange("p b (e q) -> p b e q", q=32),
+                        in1=halves[:, 2 * sel + h : 2 * sel + h + width, :, :, ((g0 + h) // 3) % 2]
+                        .rearrange("p h i q -> p (h i) q")
+                        .unsqueeze(1)
+                        .to_broadcast([P, 2, 4 * width, 32]),
+                        op=ALU.mult,
+                    )
 
         def ta_phase(p, n):
             for e in range(8):

@@ -201,10 +201,10 @@ def tile_ka_attention_heads_mod_pa_kernel(tc, x, lin_w, lin_b, grid, coef, shift
                 else:
                     nc.scalar.copy(out=dst, in_=src)
 
-        def xev_later(j, t):
+        def xev_later(j, t, on_vector=False):
             def run():
-                xev_unit(j, 2 * t, False, False)
-                xev_unit(j, 2 * t + 1, False, False)
+                xev_unit(j, 2 * t, on_vector, on_vector)
+                xev_unit(j, 2 * t + 1, on_vector, on_vector)
 
             return run
 
@@ -528,10 +528,9 @@ def tile_ka_attention_heads_mod_pa_kernel(tc, x, lin_w, lin_b, grid, coef, shift
         chains = {}
         xevs = []
         for p in range(HEAD):
-            if p < 3:
-                for fn in xevs:
-                    fn()
-                xevs = []
+            for fn in xevs:
+                fn()
+            xevs = []
             if p < 2:
                 k_phase(p + 2, nc.gpsimd)
             elif p == 2:
@@ -567,7 +566,7 @@ def tile_ka_attention_heads_mod_pa_kernel(tc, x, lin_w, lin_b, grid, coef, shift
                 quant(gxc, 0, 256, xc, xs, 512)
             for t in (2 * p, 2 * p + 1):
                 xmm(1, t)
-                xevs.extend([xev_later(1, t)])
+                xevs.extend([xev_later(1, t, p == 2)])
             if p == 2:
                 ct_last_phase(3)
 

@@ -22,7 +22,11 @@ TWO_PI = 6.283185307179586
 
 
 def plain_shift(n):
-    return n % 3 == 0
+    return n < 3 or (n >= 9 and n % 3 == 0)
+
+
+def pair_start(n):
+    return n in (3, 5, 7) or (n >= 10 and n % 3 == 1)
 
 
 def geometry(j):
@@ -43,8 +47,7 @@ def tile_ka_attention_heads_mod_pa_kernel(tc, x, lin_w, lin_b, grid, coef, shift
         ppool = ctx.enter_context(tc.tile_pool(name="ppool", bufs=3))
         opool = ctx.enter_context(tc.tile_pool(name="opool", bufs=2))
         psa = ctx.enter_context(tc.psum_pool(name="psa", bufs=2))
-        psc = ctx.enter_context(tc.psum_pool(name="psc", bufs=4))
-        psx = ctx.enter_context(tc.psum_pool(name="psx", bufs=2))
+        psc = ctx.enter_context(tc.psum_pool(name="psc", bufs=6))
 
         ident_f = const.tile([P, P], F32, name="ident_f")
         make_identity(nc, ident_f[:])
@@ -121,7 +124,7 @@ def tile_ka_attention_heads_mod_pa_kernel(tc, x, lin_w, lin_b, grid, coef, shift
             nc.sync.dma_start(out=w_sb[dc // 2][:, 5 * (dc % 2) : 5 * (dc % 2) + 5, :], in_=w_v[:, dc])
         nc.sync.dma_start(out=x_sb[:, 1:3, :], in_=x_v[:, 1:3, :])
         nc.sync.dma_start(out=x_sb[:, 4:6, :], in_=x_v[:, 4:6, :])
-        for n in range(2):
+        for n in range(3):
             sh_load(n)
         for dc in range(3):
             for kap in range(3):
@@ -164,7 +167,7 @@ def tile_ka_attention_heads_mod_pa_kernel(tc, x, lin_w, lin_b, grid, coef, shift
 
         def xmm(j, t):
             c0 = geometry(j)[1]
-            xq_of[(j, t)] = psx.tile([P, 2, 2, P], F32, name="xq")
+            xq_of[(j, t)] = psc.tile([P, 2, 2, P], F32, name="ct")
             for e in range(2):
                 ch = (2 * t + e) * P
                 for b in range(2):
@@ -499,9 +502,6 @@ def tile_ka_attention_heads_mod_pa_kernel(tc, x, lin_w, lin_b, grid, coef, shift
         empty(tp[9], c5, 0, False)
         for n in range(3):
             ct_phase(0, n)
-        sh_turn(1)
-        sh_copy(1, 0)()
-        sh_copy(1, 1)()
         open_acc(0, psa, "acc")
         open_acc(1, psa, "acc")
         open_acc(2, psc, "ct")
@@ -514,12 +514,12 @@ def tile_ka_attention_heads_mod_pa_kernel(tc, x, lin_w, lin_b, grid, coef, shift
         xmm(0, 9)
         xev_unit(0, 18, False, False)
         xev_unit(0, 19, False, False)
-        tp_y = turn(psx, "xq", x_words(1), x_words(2))
-        tp_z = turn(psx, "xq", x_words(4), x_words(5))
+        tp_y = turn(psc, "ct", x_words(1), x_words(2))
+        tp_z = turn(psc, "ct", x_words(4), x_words(5))
         for kap in range(3):
             load_coef(kap, 3, "late%d" % kap)
         sh_load(3)
-        sh_load(4)
+        sh_load(5)
         gxb = opool.tile([P, 256, 4], BF16, name="o", align_bytes=64)
         empty(tp_y, gxb, 0, False)
         gxc = opool.tile([P, 256, 4], BF16, name="o", align_bytes=64)
@@ -569,6 +569,8 @@ def tile_ka_attention_heads_mod_pa_kernel(tc, x, lin_w, lin_b, grid, coef, shift
                 xevs.extend([xev_later(1, t, p == 2)])
             if p == 2:
                 ct_last_phase(3)
+            if p == 3:
+                sh_turn(3)
 
         x_units = {HEAD: [(1, 8), (1, 9)]}
         for grp in range(2, 5):
@@ -577,8 +579,8 @@ def tile_ka_attention_heads_mod_pa_kernel(tc, x, lin_w, lin_b, grid, coef, shift
         casts = [chains[0][3]]
         late_casts = [chains[1][3]]
         evacs = [chains[2]]
-        copies = []
-        copies_later = []
+        copies = [sh_copy(3, 0)]
+        copies_later = [sh_copy(3, 1)]
         dve_small = [chains[1][1], chains[1][2]]
         for s in range(HEAD, 40):
             j, m = divmod(s, 8)
@@ -623,13 +625,14 @@ def tile_ka_attention_heads_mod_pa_kernel(tc, x, lin_w, lin_b, grid, coef, shift
                     do_ta((g - 1) // 4, (g - 1) % 2)
                     if (g - 1) % 4 == 3:
                         evacs.extend([out_chain((g - 1) // 4)])
-                if g % 12 == 0:
+                if g % 4 == 0 and pair_start(g // 4 + 1):
                     sh_turn(g // 4 + 1)
                     copies.extend([sh_copy(g // 4 + 1, 0)])
                     copies_later.extend([sh_copy(g // 4 + 1, 1)])
-                    if g // 4 + 3 < 30:
-                        sh_load(g // 4 + 3)
-                        sh_load(g // 4 + 4)
+                if g % 4 == 0 and g // 4 + 3 < 30 and g // 4 + 3 >= 9 and plain_shift(g // 4 + 3):
+                    sh_load(g // 4 + 3)
+                if g % 4 == 0 and g // 4 + 4 < 30 and g // 4 + 4 >= 7 and pair_start(g // 4 + 4):
+                    sh_load(g // 4 + 4)
                 do_m(g)
                 take = 0 if kap == 2 else ((len(dve_small) + 1) // 2 if kap == 0 else len(dve_small))
                 for fn in dve_small[:take]:

@@ -116,11 +116,14 @@ def tile_ka_attention_heads_mod_pa_kernel(tc, x, lin_w, lin_b, grid, coef, shift
 
         x_sb = coefp.tile([P, 6, 512], BF16, name="late2")
         w_sb = [coefp.tile([P, 10, 512], BF16, name="late0"), coefp.tile([P, 10, 512], BF16, name="late1")]
+        nc.sync.dma_start(out=w_sb[0][:, 0:2, :], in_=w_v[:, 0, 0:2])
+        nc.sync.dma_start(out=w_sb[0][:, 2:5, :], in_=w_v[:, 0, 2:5])
+        nc.sync.dma_start(out=w_sb[0][:, 5:6, :], in_=w_v[:, 1, 0:1])
         nc.sync.dma_start(out=x_sb[:, 0:6:3, :], in_=x_v[:, 0:6:3, :])
-        nc.sync.dma_start(out=w_sb[0][:, 0:5, :], in_=w_v[:, 0])
         nc.sync.dma_start(out=lb[0:20, :], in_=lin_b.rearrange("(t p) -> t p", p=P))
         nc.sync.dma_start(out=g_row[0:1, :], in_=grid.rearrange("(o g) f -> o (g f)", o=1))
-        for dc in range(1, 4):
+        nc.sync.dma_start(out=w_sb[0][:, 6:10, :], in_=w_v[:, 1, 1:5])
+        for dc in range(2, 4):
             nc.sync.dma_start(out=w_sb[dc // 2][:, 5 * (dc % 2) : 5 * (dc % 2) + 5, :], in_=w_v[:, dc])
         nc.sync.dma_start(out=x_sb[:, 1:3, :], in_=x_v[:, 1:3, :])
         nc.sync.dma_start(out=x_sb[:, 4:6, :], in_=x_v[:, 4:6, :])
@@ -182,7 +185,7 @@ def tile_ka_attention_heads_mod_pa_kernel(tc, x, lin_w, lin_b, grid, coef, shift
                         stop=True,
                     )
 
-        def xev_unit(j, beta, on_vector, weave_on_vector):
+        def xev_unit(j, beta, on_vector, weave_on_vector, weave_later=False):
             n, c0, a = geometry(j)
             dc, cc = divmod(beta, 5)
             if beta == 0:
@@ -196,13 +199,18 @@ def tile_ka_attention_heads_mod_pa_kernel(tc, x, lin_w, lin_b, grid, coef, shift
                 nc.vector.tensor_scalar(out=dst, in0=src, scalar1=bias, scalar2=None, op0=ALU.add)
             else:
                 nc.scalar.activation(out=dst, in_=src, func=ACT.Identity, bias=bias, scale=1.0)
-            if cc == 4:
-                dst = xt[j][:, :, dc, 0 : 5 * n].rearrange("p b (r c) -> p b r c", c=5)
-                src = cur["tmp"][:, :, :, 0:n].rearrange("p c b r -> p b r c")
+            woven = xt[j][:, :, dc, 0 : 5 * n].rearrange("p b (r c) -> p b r c", c=5)
+            staged = cur["tmp"][:, :, :, 0:n].rearrange("p c b r -> p b r c")
+
+            def weave():
                 if weave_on_vector:
-                    nc.vector.tensor_copy(out=dst, in_=src)
+                    nc.vector.tensor_copy(out=woven, in_=staged)
                 else:
-                    nc.scalar.copy(out=dst, in_=src)
+                    nc.scalar.copy(out=woven, in_=staged)
+
+            if cc == 4 and not weave_later:
+                weave()
+            return weave
 
         def xev_later(j, t, on_vector=False):
             def run():
@@ -431,27 +439,27 @@ def tile_ka_attention_heads_mod_pa_kernel(tc, x, lin_w, lin_b, grid, coef, shift
                     stop=(p == 3 and e == 7),
                 )
 
-        tp_x = turn(psc, "ct", x_words(0), x_words(3))
         tp = {}
         for i in range(3):
             tp[i] = turn(psc, "ct", w_words(2 * i), w_words(2 * i + 1))
-        gxa = chunk(256)
-        empty(tp_x, gxa, 0, True)
+        tp_x = turn(psc, "ct", x_words(0), x_words(3))
         c0 = chunk(512)
         empty(tp[0], c0, 0, False)
         empty(tp[1], c0, 256, True)
+        quant(c0, 0, 512, wc, ws, 0)
         c1 = chunk(256)
         empty(tp[2], c1, 0, False)
+        gxa = chunk(256)
+        empty(tp_x, gxa, 0, True)
+        quant(c1, 0, 256, wc, ws, 512)
+        quant(gxa, 0, 128, xc, xs, 0)
+        quant(gxa, 128, 256, xc, xs, 384)
         tb = psc.tile([P, P], BF16, name="ct")
         nc.tensor.transpose(tb[:], lb[:], ident_b[:])
         nc.vector.tensor_copy(out=bias_t[:], in_=tb[:, 0:20])
         gp = psc.tile([P, 40], F32, name="ct")
         nc.tensor.matmul(out=gp[:], lhsT=first_row[:], rhs=g_row[:], start=True, stop=True)
         nc.vector.tensor_scalar(out=gsc[:], in0=gp[:], scalar1=1.0 / TWO_PI, scalar2=None, op0=ALU.mult)
-        quant(gxa, 0, 128, xc, xs, 0)
-        quant(gxa, 128, 256, xc, xs, 384)
-        quant(c0, 0, 512, wc, ws, 0)
-        quant(c1, 0, 256, wc, ws, 512)
         tp[3] = turn(psc, "ct", w_words(6), w_words(7))
         tp[4] = turn(psc, "ct", w_words(8), w_words(9))
         xmm(0, 0)
@@ -528,6 +536,10 @@ def tile_ka_attention_heads_mod_pa_kernel(tc, x, lin_w, lin_b, grid, coef, shift
         chains = {}
         xevs = []
         for p in range(HEAD):
+            if p == 3:
+                xevs = []
+                xev_unit(1, 8, True, True)
+                weave_1 = xev_unit(1, 9, True, True, True)
             for fn in xevs:
                 fn()
             xevs = []
@@ -536,6 +548,10 @@ def tile_ka_attention_heads_mod_pa_kernel(tc, x, lin_w, lin_b, grid, coef, shift
             elif p == 2:
                 do_k(p + 2)
             for n in range(3):
+                if p == 3 and n == 2:
+                    weave_1()
+                    xev_unit(1, 10, True, True)
+                    xev_unit(1, 11, True, True)
                 m_phase(p, n)
                 ta_phase(p, n)
                 if p < 2:
@@ -554,8 +570,8 @@ def tile_ka_attention_heads_mod_pa_kernel(tc, x, lin_w, lin_b, grid, coef, shift
             elif p == 2:
                 do_k(HEAD + 1)
                 do_r(HEAD)
-                do_r(HEAD + 1)
             else:
+                do_r(HEAD + 1)
                 chains[0][1]()
                 chains[0][2]()
                 for fn in xevs:

@@ -239,7 +239,10 @@ def tile_ka_attention_heads_mod_pa_kernel(tc, x, lin_w, lin_b, grid, coef, shift
                 op1=ALU.add,
             )
 
-        def do_r(s):
+        def do_sin(s):
+            nc.scalar.activation(out=s_of[s][:], in_=s_of[s][:], func=ACT.Sin, scale=TWO_PI)
+
+        def do_r(s, sine_later=False):
             r_done[s] = True
             j = s // 8
             o = 384 * j - 5 * ((384 * j) // 5)
@@ -251,7 +254,8 @@ def tile_ka_attention_heads_mod_pa_kernel(tc, x, lin_w, lin_b, grid, coef, shift
                 op0=ALU.mult,
                 op1=ALU.subtract,
             )
-            nc.scalar.activation(out=s_of[s][:], in_=s_of[s][:], func=ACT.Sin, scale=TWO_PI)
+            if not sine_later:
+                do_sin(s)
 
         def do_ct(g):
             j, q = divmod(g, 24)
@@ -552,6 +556,8 @@ def tile_ka_attention_heads_mod_pa_kernel(tc, x, lin_w, lin_b, grid, coef, shift
                     weave_1()
                     xev_unit(1, 10, True, True)
                     xev_unit(1, 11, True, True)
+                    chains[0][1]()
+                    chains[0][2]()
                 m_phase(p, n)
                 ta_phase(p, n)
                 if p < 2:
@@ -571,9 +577,7 @@ def tile_ka_attention_heads_mod_pa_kernel(tc, x, lin_w, lin_b, grid, coef, shift
                 do_k(HEAD + 1)
                 do_r(HEAD)
             else:
-                do_r(HEAD + 1)
-                chains[0][1]()
-                chains[0][2]()
+                do_r(HEAD + 1, True)
                 for fn in xevs:
                     fn()
                 xevs = []
@@ -616,6 +620,8 @@ def tile_ka_attention_heads_mod_pa_kernel(tc, x, lin_w, lin_b, grid, coef, shift
             copies_later = []
             xevs = []
             dve_small.extend(new_small)
+            if s == HEAD:
+                do_sin(HEAD + 1)
             if s + 1 < 40 and s + 1 not in r_done:
                 do_r(s + 1)
             if s + 2 < 40 and (s + 2, 0) not in kt_of:

@@ -541,9 +541,9 @@ def tile_ka_attention_heads_mod_pa_kernel(tc, x, lin_w, lin_b, grid, coef, shift
         xevs = []
         for p in range(HEAD):
             if p == 3:
-                xevs = []
-                xev_unit(1, 8, True, True)
-                weave_1 = xev_unit(1, 9, True, True, True)
+                xevs = [xev_later(1, 5)]
+                xev_unit(1, 8, True, False)
+                xev_unit(1, 9, True, False)
             for fn in xevs:
                 fn()
             xevs = []
@@ -552,12 +552,6 @@ def tile_ka_attention_heads_mod_pa_kernel(tc, x, lin_w, lin_b, grid, coef, shift
             elif p == 2:
                 do_k(p + 2)
             for n in range(3):
-                if p == 3 and n == 2:
-                    weave_1()
-                    xev_unit(1, 10, True, True)
-                    xev_unit(1, 11, True, True)
-                    chains[0][1]()
-                    chains[0][2]()
                 m_phase(p, n)
                 ta_phase(p, n)
                 if p < 2:
@@ -578,6 +572,8 @@ def tile_ka_attention_heads_mod_pa_kernel(tc, x, lin_w, lin_b, grid, coef, shift
                 do_r(HEAD)
             else:
                 do_r(HEAD + 1, True)
+                chains[0][1]()
+                chains[0][2]()
                 for fn in xevs:
                     fn()
                 xevs = []
@@ -604,6 +600,9 @@ def tile_ka_attention_heads_mod_pa_kernel(tc, x, lin_w, lin_b, grid, coef, shift
         dve_small = [chains[1][1], chains[1][2]]
         for s in range(HEAD, 40):
             j, m = divmod(s, 8)
+            if s == HEAD:
+                for fn in copies + xevs:
+                    fn()
             for fn in casts:
                 fn()
             new_small = []
@@ -612,8 +611,9 @@ def tile_ka_attention_heads_mod_pa_kernel(tc, x, lin_w, lin_b, grid, coef, shift
                 new_small.extend([fns[1], fns[2]])
             cast_next = late_casts + [fns[3] for fns in evacs]
             late_casts = []
-            for fn in copies + xevs:
-                fn()
+            if s > HEAD:
+                for fn in copies + xevs:
+                    fn()
             casts = cast_next
             evacs = []
             copies = copies_later

@@ -127,8 +127,6 @@ def tile_ka_attention_heads_mod_pa_kernel(tc, x, lin_w, lin_b, grid, coef, shift
             nc.sync.dma_start(out=w_sb[dc // 2][:, 5 * (dc % 2) : 5 * (dc % 2) + 5, :], in_=w_v[:, dc])
         nc.sync.dma_start(out=x_sb[:, 1:3, :], in_=x_v[:, 1:3, :])
         nc.sync.dma_start(out=x_sb[:, 4:6, :], in_=x_v[:, 4:6, :])
-        for n in range(3):
-            sh_load(n)
         for dc in range(3):
             for kap in range(3):
                 load_coef(kap, dc, "cn%d_%d" % (kap, dc))
@@ -303,6 +301,8 @@ def tile_ka_attention_heads_mod_pa_kernel(tc, x, lin_w, lin_b, grid, coef, shift
 
         def open_acc(n, pool, name):
             acc_of[n] = pool.tile([P, 512], F32, name=name)
+            if n < 3:
+                return
             if plain_shift(n):
                 nc.tensor.matmul(out=acc_of[n][:], lhsT=ident_b[:], rhs=sh_of[n][:], start=True, stop=False)
             for dc in range(0 if plain_shift(n) else 4):
@@ -439,9 +439,11 @@ def tile_ka_attention_heads_mod_pa_kernel(tc, x, lin_w, lin_b, grid, coef, shift
                     lhsT=pth[n][:, e].rearrange("p a q -> p (a q)"),
                     rhs=ident_f[:],
                     is_transpose=True,
-                    start=False,
-                    stop=(p == 3 and e == 7),
+                    start=(p == 0 and e == 0),
+                    stop=False,
                 )
+            if p == 3:
+                nc.tensor.matmul(out=acc_of[n][:], lhsT=ident_b[:], rhs=sh_of[n][:], start=False, stop=True)
 
         tp = {}
         for i in range(3):
@@ -530,8 +532,8 @@ def tile_ka_attention_heads_mod_pa_kernel(tc, x, lin_w, lin_b, grid, coef, shift
         tp_z = turn(psc, "ct", x_words(4), x_words(5))
         for kap in range(3):
             load_coef(kap, 3, "late%d" % kap)
-        sh_load(3)
-        sh_load(5)
+        for n in (0, 1, 2, 3, 5):
+            sh_load(n)
         gxb = opool.tile([P, 256, 4], BF16, name="o", align_bytes=64)
         empty(tp_y, gxb, 0, False)
         gxc = opool.tile([P, 256, 4], BF16, name="o", align_bytes=64)

@@ -22,11 +22,11 @@ TWO_PI = 6.283185307179586
 
 
 def plain_shift(n):
-    return n < 3 or (n >= 9 and n % 3 == 0)
+    return n < 10
 
 
 def pair_start(n):
-    return n in (3, 5, 7) or (n >= 10 and n % 3 == 1)
+    return 10 <= n < 30 and n % 2 == 0
 
 
 def geometry(j):
@@ -532,7 +532,7 @@ def tile_ka_attention_heads_mod_pa_kernel(tc, x, lin_w, lin_b, grid, coef, shift
         tp_z = turn(psc, "ct", x_words(4), x_words(5))
         for kap in range(3):
             load_coef(kap, 3, "late%d" % kap)
-        for n in (0, 1, 2, 3, 5):
+        for n in range(6):
             sh_load(n)
         gxb = opool.tile([P, 256, 4], BF16, name="o", align_bytes=64)
         empty(tp_y, gxb, 0, False)
@@ -587,8 +587,6 @@ def tile_ka_attention_heads_mod_pa_kernel(tc, x, lin_w, lin_b, grid, coef, shift
                 xevs.extend([xev_later(1, t, p == 2)])
             if p == 2:
                 ct_last_phase(3)
-            if p == 3:
-                sh_turn(3)
 
         x_units = {HEAD: [(1, 8), (1, 9)]}
         for grp in range(2, 5):
@@ -597,8 +595,8 @@ def tile_ka_attention_heads_mod_pa_kernel(tc, x, lin_w, lin_b, grid, coef, shift
         casts = [chains[0][3]]
         late_casts = [chains[1][3]]
         evacs = [chains[2]]
-        copies = [sh_copy(3, 0)]
-        copies_later = [sh_copy(3, 1)]
+        copies = []
+        copies_later = []
         dve_small = [chains[1][1], chains[1][2]]
         for s in range(HEAD, 40):
             j, m = divmod(s, 8)
@@ -653,10 +651,8 @@ def tile_ka_attention_heads_mod_pa_kernel(tc, x, lin_w, lin_b, grid, coef, shift
                     sh_turn(g // 4 + 1)
                     copies.extend([sh_copy(g // 4 + 1, 0)])
                     copies_later.extend([sh_copy(g // 4 + 1, 1)])
-                if g % 4 == 0 and g // 4 + 3 < 30 and g // 4 + 3 >= 9 and plain_shift(g // 4 + 3):
-                    sh_load(g // 4 + 3)
-                if g % 4 == 0 and g // 4 + 4 < 30 and g // 4 + 4 >= 7 and pair_start(g // 4 + 4):
-                    sh_load(g // 4 + 4)
+                if g % 4 == 0 and 6 <= g // 4 + 2 < 30 and (plain_shift(g // 4 + 2) or pair_start(g // 4 + 2)):
+                    sh_load(g // 4 + 2)
                 do_m(g)
                 take = 0 if kap == 2 else ((len(dve_small) + 1) // 2 if kap == 0 else len(dve_small))
                 for fn in dve_small[:take]:

@@ -117,9 +117,10 @@ def tile_ka_attention_heads_mod_pa_kernel(tc, x, lin_w, lin_b, grid, coef, shift
         x_sb = coefp.tile([P, 6, 512], BF16, name="late2")
         w_sb = [coefp.tile([P, 10, 512], BF16, name="late0"), coefp.tile([P, 10, 512], BF16, name="late1")]
         nc.sync.dma_start(out=w_sb[0][:, 0:2, :], in_=w_v[:, 0, 0:2])
-        nc.sync.dma_start(out=w_sb[0][:, 2:5, :], in_=w_v[:, 0, 2:5])
-        nc.sync.dma_start(out=w_sb[0][:, 5:6, :], in_=w_v[:, 1, 0:1])
         nc.sync.dma_start(out=x_sb[:, 0:6:3, :], in_=x_v[:, 0:6:3, :])
+        nc.sync.dma_start(out=w_sb[0][:, 2:4, :], in_=w_v[:, 0, 2:4])
+        nc.sync.dma_start(out=w_sb[0][:, 4:5, :], in_=w_v[:, 0, 4:5])
+        nc.sync.dma_start(out=w_sb[0][:, 5:6, :], in_=w_v[:, 1, 0:1])
         nc.sync.dma_start(out=lb[0:20, :], in_=lin_b.rearrange("(t p) -> t p", p=P))
         nc.sync.dma_start(out=g_row[0:1, :], in_=grid.rearrange("(o g) f -> o (g f)", o=1))
         nc.sync.dma_start(out=w_sb[0][:, 6:10, :], in_=w_v[:, 1, 1:5])
@@ -365,20 +366,21 @@ def tile_ka_attention_heads_mod_pa_kernel(tc, x, lin_w, lin_b, grid, coef, shift
 
             return evac, amax, recip, cast
 
-        def k_phase(p, eng):
+        def k_one(p, m, eng):
+            eng.tensor_scalar(
+                out=kph[p][:, :, m, :],
+                in0=xt[0][:, :, p, 0:384],
+                scalar1=gsc[:, m : m + 1],
+                scalar2=0.0,
+                op0=ALU.mult,
+                op1=ALU.add,
+            )
+
+        def k_phase(p, eng, count=4):
             sph[p] = spool.tile([P, 2, 4, 384], F32, name="st")
             kph[p] = sph[p][:].bitcast(I32)
-            for half in range(2):
-                for mm in range(2):
-                    m = 2 * half + mm
-                    eng.tensor_scalar(
-                        out=kph[p][:, :, m, :],
-                        in0=xt[0][:, :, p, 0:384],
-                        scalar1=gsc[:, m : m + 1],
-                        scalar2=0.0,
-                        op0=ALU.mult,
-                        op1=ALU.add,
-                    )
+            for m in range(count):
+                k_one(p, m, eng)
 
         def r_phase(p, half):
             for mm in range(2):
@@ -446,20 +448,21 @@ def tile_ka_attention_heads_mod_pa_kernel(tc, x, lin_w, lin_b, grid, coef, shift
                 nc.tensor.matmul(out=acc_of[n][:], lhsT=ident_b[:], rhs=sh_of[n][:], start=False, stop=True)
 
         tp = {}
-        for i in range(3):
-            tp[i] = turn(psc, "ct", w_words(2 * i), w_words(2 * i + 1))
+        tp[0] = turn(psc, "ct", w_words(0), w_words(1))
         tp_x = turn(psc, "ct", x_words(0), x_words(3))
+        tp[1] = turn(psc, "ct", w_words(2), w_words(3))
+        tp[2] = turn(psc, "ct", w_words(4), w_words(5))
         c0 = chunk(512)
         empty(tp[0], c0, 0, False)
-        empty(tp[1], c0, 256, True)
+        gxa = chunk(256)
+        empty(tp_x, gxa, 0, True)
+        quant(gxa, 0, 128, xc, xs, 0)
+        quant(gxa, 128, 256, xc, xs, 384)
+        empty(tp[1], c0, 256, False)
         quant(c0, 0, 512, wc, ws, 0)
         c1 = chunk(256)
         empty(tp[2], c1, 0, False)
-        gxa = chunk(256)
-        empty(tp_x, gxa, 0, True)
         quant(c1, 0, 256, wc, ws, 512)
-        quant(gxa, 0, 128, xc, xs, 0)
-        quant(gxa, 128, 256, xc, xs, 384)
         tb = psc.tile([P, P], BF16, name="ct")
         nc.tensor.transpose(tb[:], lb[:], ident_b[:])
         nc.vector.tensor_copy(out=bias_t[:], in_=tb[:, 0:20])
@@ -550,7 +553,7 @@ def tile_ka_attention_heads_mod_pa_kernel(tc, x, lin_w, lin_b, grid, coef, shift
                 fn()
             xevs = []
             if p < 2:
-                k_phase(p + 2, nc.gpsimd)
+                k_phase(p + 2, nc.gpsimd, 3)
             elif p == 2:
                 do_k(p + 2)
             for n in range(3):
@@ -567,6 +570,7 @@ def tile_ka_attention_heads_mod_pa_kernel(tc, x, lin_w, lin_b, grid, coef, shift
             if p < 2:
                 r_phase(p + 2, 0)
                 sin_phase(p + 2, 0)
+                k_one(p + 2, 3, nc.vector)
                 r_phase(p + 2, 1)
                 sin_phase(p + 2, 1)
             elif p == 2:

@@ -256,6 +256,20 @@ def tile_ka_attention_heads_mod_pa_kernel(tc, x, lin_w, lin_b, grid, coef, shift
             if not sine_later:
                 do_sin(s)
 
+        def do_r_third(s, kap):
+            j = s // 8
+            o = 384 * j - 5 * ((384 * j) // 5)
+            part = s_of[s][:, :, :, kap * P : (kap + 1) * P]
+            nc.vector.scalar_tensor_tensor(
+                out=part,
+                in0=xt[j][:, :, :, o + kap * P : o + (kap + 1) * P],
+                scalar=gsc[:, s : s + 1],
+                in1=kt_of[s][:, :, :, kap * P : (kap + 1) * P],
+                op0=ALU.mult,
+                op1=ALU.subtract,
+            )
+            nc.scalar.activation(out=part, in_=part, func=ACT.Sin, scale=TWO_PI)
+
         def do_ct(g):
             j, q = divmod(g, 24)
             m, kap = divmod(q, 3)
@@ -364,7 +378,16 @@ def tile_ka_attention_heads_mod_pa_kernel(tc, x, lin_w, lin_b, grid, coef, shift
                 )
                 nc.sync.dma_start(out=out1_v[:, rows, :], in_=t["f8"][:].bitcast(U8))
 
-            return evac, amax, recip, cast
+            def cast_on_vector():
+                t["rs"] = opool.tile([P, 1], F32, name="rs")
+                nc.vector.tensor_scalar(out=t["rs"][:], in0=t["rc"][:], scalar1=448.0, scalar2=None, op0=ALU.mult)
+                t["f8"] = opool.tile([P, 512], FP8, name="f8")
+                nc.vector.tensor_scalar(
+                    out=t["f8"][:], in0=t["o"][:], scalar1=t["rs"][:, 0:1], scalar2=None, op0=ALU.mult, saturate=False
+                )
+                nc.sync.dma_start(out=out1_v[:, rows, :], in_=t["f8"][:].bitcast(U8))
+
+            return evac, amax, recip, cast, cast_on_vector
 
         def k_one(p, m, eng):
             eng.tensor_scalar(
@@ -602,7 +625,7 @@ def tile_ka_attention_heads_mod_pa_kernel(tc, x, lin_w, lin_b, grid, coef, shift
         copies = []
         copies_later = []
         dve_small = [chains[1][1], chains[1][2]]
-        for s in range(HEAD, 40):
+        for s in range(HEAD, 39):
             j, m = divmod(s, 8)
             if s == HEAD:
                 for fn in copies + xevs:
@@ -626,24 +649,11 @@ def tile_ka_attention_heads_mod_pa_kernel(tc, x, lin_w, lin_b, grid, coef, shift
             dve_small.extend(new_small)
             if s == HEAD:
                 do_sin(HEAD + 1)
-            if s + 1 < 40 and s + 1 not in r_done:
+            if s + 1 < 39 and s + 1 not in r_done:
                 do_r(s + 1)
             if s + 2 < 40 and (s + 2, 0) not in kt_of:
                 do_k(s + 2)
-            if s == 39:
-                do_ct(119)
-                do_m(118)
-                take = (len(dve_small) + 1) // 2
-                for fn in dve_small[:take]:
-                    fn()
-                dve_small = dve_small[take:]
-                do_ta(29, 0)
-                do_m(117)
-                for fn in dve_small:
-                    fn()
-                dve_small = []
-                do_m(119)
-            for kap in range(3 if s < 39 else 0):
+            for kap in range(3 if s < 38 else 0):
                 g = 3 * s + kap
                 if g + 2 < 120:
                     do_ct(g + 2)
@@ -665,13 +675,34 @@ def tile_ka_attention_heads_mod_pa_kernel(tc, x, lin_w, lin_b, grid, coef, shift
             for grp, t in x_units.get(s, []):
                 xmm(grp, t)
                 xevs.extend([xev_later(grp, t)])
-        do_ta(29, 1)
-        last = out_chain(29)
+        do_ct(116)
+        do_ct(118)
+        do_m(114)
+        do_r_third(39, 1)
+        do_ta(28, 0)
+        do_ct(117)
+        do_m(115)
         for fn in dve_small:
             fn()
+        do_ta(28, 1)
+        before_last = out_chain(28)
+        do_ct(119)
+        do_m(116)
         for fn in casts:
             fn()
+        do_m(118)
+        do_ta(29, 0)
+        do_r_third(39, 0)
+        do_r_third(39, 2)
+        before_last[0]()
+        do_m(117)
+        do_m(119)
+        do_ta(29, 1)
+        before_last[1]()
+        before_last[2]()
+        last = out_chain(29)
         last[0]()
+        before_last[3]()
         last[1]()
         last[2]()
-        last[3]()
+        last[4]()

@@ -22,11 +22,11 @@ TWO_PI = 6.283185307179586
 
 
 def plain_shift(n):
-    return n < 10
+    return n < 8 or n >= 28
 
 
 def pair_start(n):
-    return 10 <= n < 30 and n % 2 == 0
+    return 8 <= n < 28 and n % 2 == 0
 
 
 def geometry(j):

@@ -299,6 +299,30 @@ def tile_ka_attention_heads_mod_pa_kernel(tc, x, lin_w, lin_b, grid, coef, shift
                     op=ALU.mult,
                 )
 
+        def coef_to_sbuf(g):
+            j, q = divmod(g, 24)
+            m = q // 3
+            cur["cf"] = opool.tile([P, 4, P], BF16, name="sh", bufs=3)
+            nc.scalar.copy(
+                out=cur["cf"][:],
+                in_=ct_of[g][:].bitcast(BF16).rearrange("p c (r t) -> p c r t", t=2)[:, :, :, (m * 5 + j) % 2],
+            )
+
+        def do_m_gpsimd(g):
+            j, q = divmod(g, 24)
+            m, kap = divmod(q, 3)
+            sel = (q % 4) // 2
+            h = q % 2
+            if sel == 0:
+                pt[h] = ppool.tile([P, 4, 4, 4, 32], F32, name="pt", align_bytes=64)
+            nc.vector.memset(pt[h][:, 0, 0, sel : sel + 1, 0:1], 0.0)
+            nc.gpsimd.tensor_tensor(
+                out=pt[h][:].rearrange("p c i (b s) q -> p b c i s q", b=2)[:, :, :, :, sel, :],
+                in0=s_of[j * 8 + m][:, :, :, kap * P : (kap + 1) * P].rearrange("p b c (i q) -> p b c i q", i=4),
+                in1=cur["cf"][:].rearrange("p c (i q) -> p c i q", i=4).unsqueeze(1).to_broadcast([P, 2, 4, 4, 32]),
+                op=ALU.mult,
+            )
+
         def sh_turn(n):
             cts_of[n] = psc.tile([P, 4, P], BF16, name="ct")
             for dc in range(4):
@@ -677,9 +701,11 @@ def tile_ka_attention_heads_mod_pa_kernel(tc, x, lin_w, lin_b, grid, coef, shift
                 xevs.extend([xev_later(grp, t)])
         do_ct(116)
         do_ct(118)
+        coef_to_sbuf(116)
         do_m(114)
         do_r_third(39, 1)
         do_ta(28, 0)
+        do_m_gpsimd(116)
         do_ct(117)
         do_m(115)
         for fn in dve_small:
@@ -687,7 +713,6 @@ def tile_ka_attention_heads_mod_pa_kernel(tc, x, lin_w, lin_b, grid, coef, shift
         do_ta(28, 1)
         before_last = out_chain(28)
         do_ct(119)
-        do_m(116)
         for fn in casts:
             fn()
         do_m(118)

from contextlib import ExitStack

import concourse.mybir as mybir
from concourse.masks import make_identity

FLOPS = 2 * 768 * 2560 * 512

F32 = mybir.dt.float32
BF16 = mybir.dt.bfloat16
I32 = mybir.dt.int32
U32 = mybir.dt.uint32
U8 = mybir.dt.uint8
FP8X4 = mybir.dt.float8_e4m3fn_x4
FP8 = mybir.dt.float8_e4m3fn
ALU = mybir.AluOpType
ACT = mybir.ActivationFunctionType
AX = mybir.AxisListType

P = 128
HEAD = 4
TWO_PI = 6.283185307179586


def plain_shift(n):
    return n < 8 or n >= 28


def pair_start(n):
    return 8 <= n < 28 and n % 2 == 0


def geometry(j):
    r_lo = (384 * j) // 5
    n = (384 * j + 383) // 5 + 1 - r_lo
    c0 = r_lo // 64
    return n, c0, r_lo - 64 * c0


def tile_ka_attention_heads_mod_pa_kernel(tc, x, lin_w, lin_b, grid, coef, shift, out_0, out_1):
    nc = tc.nc
    with ExitStack() as ctx:
        const = ctx.enter_context(tc.tile_pool(name="const", bufs=1))
        coefp = ctx.enter_context(tc.tile_pool(name="coefp", bufs=1))
        xpool = ctx.enter_context(tc.tile_pool(name="xpool", bufs=2))
        tpool = ctx.enter_context(tc.tile_pool(name="tpool", bufs=1))
        spool = ctx.enter_context(tc.tile_pool(name="spool", bufs=3))
        ppool = ctx.enter_context(tc.tile_pool(name="ppool", bufs=3))
        opool = ctx.enter_context(tc.tile_pool(name="opool", bufs=2))
        psa = ctx.enter_context(tc.psum_pool(name="psa", bufs=2))
        psc = ctx.enter_context(tc.psum_pool(name="psc", bufs=6))

        ident_f = const.tile([P, P], F32, name="ident_f")
        make_identity(nc, ident_f[:])
        ident_b = const.tile([P, P], BF16, name="ident_b")
        make_identity(nc, ident_b[:])
        zero_col = const.tile([P, 1], F32, name="zero_col")
        nc.vector.memset(zero_col[:], 0.0)
        warm = const.tile([P, 1], F32, name="warm")
        nc.scalar.activation(out=warm[:], in_=zero_col[:], func=ACT.Sin)

        wc = const.tile([P, 2560], U32, name="wc", align_bytes=64)
        ws = const.tile([P, 2560], U8, name="ws", align_bytes=64)
        xc = const.tile([P, 768], U32, name="xc", align_bytes=64)
        xs = const.tile([P, 768], U8, name="xs", align_bytes=64)
        gsc = const.tile([P, 40], F32, name="gsc")
        bias_t = const.tile([P, 20], F32, name="bias_t")
        lb = const.tile([P, P], BF16, name="lb")
        nc.vector.memset(lb[:], 0.0)
        g_row = const.tile([P, 40], BF16, name="g_row")
        nc.vector.memset(g_row[:], 0.0)
        first_row = const.tile([P, P], BF16, name="first_row")
        nc.vector.memset(first_row[:], 0.0)
        nc.vector.memset(first_row[0:1, :], 1.0)

        ctx.enter_context(tc.manual_schedule())

        out0_v = out_0.rearrange("b h g p d -> b (h g p) d")
        out1_v = out_1.rearrange("b h g p d -> b (h g p) d")
        shift_v = shift.rearrange("o h g p d -> (o h g p) d")
        coef_v = coef.rearrange("(r d) m j -> r d (m j)", d=512)
        x_v = x.rearrange("b h p d -> (b h p) d").rearrange("(t p) d -> p t d", p=P)
        w_v = lin_w.rearrange("(c q p) k -> p q c k", q=4, p=P)

        cn = {}
        xt = {}
        xq_of = {}
        kt_of = {}
        r_done = {}
        s_of = {}
        ct_of = {}
        pt = {}
        sh_of = {}
        cts_of = {}
        sht_of = {}
        acc_of = {}
        cur = {}
        kph = {}
        sph = {}
        cth = {}
        pth = {}

        def load_coef(kap, dc, name):
            cn[(kap, dc)] = coefp.tile([P, P, 40], BF16, name=name)
            nc.sync.dma_start(
                out=cn[(kap, dc)][:],
                in_=coef_v[kap * P : (kap + 1) * P, dc * P : (dc + 1) * P, :],
            )

        def sh_load(n):
            sh_of[n] = opool.tile([P, 512], BF16, name="sh", bufs=3)
            if plain_shift(n):
                for b in range(2):
                    nc.sync.dma_start(out=sh_of[n][b * 64 : (b + 1) * 64, :], in_=shift_v[n * 64 : (n + 1) * 64, :])
            else:
                nc.sync.dma_start(out=sh_of[n][:], in_=shift_v[n * 64 : (n + 2) * 64, :])

        x_sb = coefp.tile([P, 6, 512], BF16, name="late2")
        w_sb = [coefp.tile([P, 10, 512], BF16, name="late0"), coefp.tile([P, 10, 512], BF16, name="late1")]
        nc.sync.dma_start(out=w_sb[0][:, 0:2, :], in_=w_v[:, 0, 0:2])
        nc.sync.dma_start(out=x_sb[:, 0:6:3, :], in_=x_v[:, 0:6:3, :])
        nc.sync.dma_start(out=w_sb[0][:, 2:4, :], in_=w_v[:, 0, 2:4])
        nc.sync.dma_start(out=w_sb[0][:, 4:5, :], in_=w_v[:, 0, 4:5])
        nc.sync.dma_start(out=w_sb[0][:, 5:6, :], in_=w_v[:, 1, 0:1])
        nc.sync.dma_start(out=lb[0:20, :], in_=lin_b.rearrange("(t p) -> t p", p=P))
        nc.sync.dma_start(out=g_row[0:1, :], in_=grid.rearrange("(o g) f -> o (g f)", o=1))
        nc.sync.dma_start(out=w_sb[0][:, 6:10, :], in_=w_v[:, 1, 1:5])
        for dc in range(2, 4):
            nc.sync.dma_start(out=w_sb[dc // 2][:, 5 * (dc % 2) : 5 * (dc % 2) + 5, :], in_=w_v[:, dc])
        nc.sync.dma_start(out=x_sb[:, 1:3, :], in_=x_v[:, 1:3, :])
        nc.sync.dma_start(out=x_sb[:, 4:6, :], in_=x_v[:, 4:6, :])
        for dc in range(3):
            for kap in range(3):
                load_coef(kap, dc, "cn%d_%d" % (kap, dc))

        x32 = x_sb[:].bitcast(F32)
        w32 = [w_sb[0][:].bitcast(F32), w_sb[1][:].bitcast(F32)]

        def x_words(t):
            return x32[:, t, :]

        def w_words(beta):
            return w32[beta // 10][:, beta % 10, :]

        def turn(pool, name, words_a, words_b):
            tp = pool.tile([P, 2, 2, P], F32, name=name)
            for e in range(2):
                words = words_a if e == 0 else words_b
                for u in range(2):
                    nc.tensor.transpose(tp[:, e, u, :], words[:, u:256:2], ident_f[:])
            return tp

        def chunk(rows):
            return ppool.tile([P, rows, 4], BF16, name="pt", align_bytes=64)

        def empty(tp, grouped, lo, on_vector):
            dst = grouped[:].bitcast(F32)[:, lo : lo + 2 * P, :].rearrange("p (e r) u -> p e r u", e=2)
            src = tp[:].rearrange("p e u r -> p e r u")
            if on_vector:
                nc.vector.tensor_copy(out=dst, in_=src)
            else:
                nc.scalar.copy(out=dst, in_=src)

        def quant(grouped, lo, hi, codes, scales, col):
            nc.vector.quantize_mx(
                out=codes[:, col : col + hi - lo].bitcast(FP8X4),
                scales=scales[:, col : col + hi - lo],
                in_=grouped[:, lo:hi, :].rearrange("p r t -> p (r t)"),
            )

        def xmm(j, t):
            c0 = geometry(j)[1]
            xq_of[(j, t)] = psc.tile([P, 2, 2, P], F32, name="ct")
            for e in range(2):
                ch = (2 * t + e) * P
                for b in range(2):
                    col = b * 384 + c0 * 64
                    nc.tensor.matmul_mx(
                        out=xq_of[(j, t)][:, e, b, :],
                        lhsT=wc[:, ch : ch + P].bitcast(FP8X4),
                        lhsT_scale=ws[:, ch : ch + P],
                        rhs=xc[:, col : col + P].bitcast(FP8X4),
                        rhs_scale=xs[:, col : col + P],
                        start=True,
                        stop=True,
                    )

        def xev_unit(j, beta, on_vector, weave_on_vector, weave_later=False):
            n, c0, a = geometry(j)
            dc, cc = divmod(beta, 5)
            if beta == 0:
                xt[j] = xpool.tile([P, 2, 4, 400], F32, name="xt", align_bytes=64)
            if cc == 0:
                cur["tmp"] = tpool.tile([P, 5, 2, 78], F32, name="tmp")
            src = xq_of[(j, beta // 2)][:, beta % 2, :, a : a + n]
            dst = cur["tmp"][:, cc, :, 0:n]
            bias = bias_t[:, cc * 4 + dc : cc * 4 + dc + 1]
            if on_vector:
                nc.vector.tensor_scalar(out=dst, in0=src, scalar1=bias, scalar2=None, op0=ALU.add)
            else:
                nc.scalar.activation(out=dst, in_=src, func=ACT.Identity, bias=bias, scale=1.0)
            woven = xt[j][:, :, dc, 0 : 5 * n].rearrange("p b (r c) -> p b r c", c=5)
            staged = cur["tmp"][:, :, :, 0:n].rearrange("p c b r -> p b r c")

            def weave():
                if weave_on_vector:
                    nc.vector.tensor_copy(out=woven, in_=staged)
                else:
                    nc.scalar.copy(out=woven, in_=staged)

            if cc == 4 and not weave_later:
                weave()
            return weave

        def xev_later(j, t, on_vector=False):
            def run():
                xev_unit(j, 2 * t, on_vector, on_vector)
                xev_unit(j, 2 * t + 1, on_vector, on_vector)

            return run

        def x_slice(s, b):
            j = s // 8
            o = 384 * j - 5 * ((384 * j) // 5)
            return xt[j][:, b, :, o : o + 384]

        def do_k(s):
            j = s // 8
            o = 384 * j - 5 * ((384 * j) // 5)
            s_of[s] = spool.tile([P, 2, 4, 384], F32, name="st")
            kt_of[s] = s_of[s][:].bitcast(I32)
            kt_of[(s, 0)] = True
            nc.gpsimd.tensor_scalar(
                out=kt_of[s],
                in0=xt[j][:, :, :, o : o + 384],
                scalar1=gsc[:, s : s + 1],
                scalar2=0.0,
                op0=ALU.mult,
                op1=ALU.add,
            )

        def do_sin(s):
            nc.scalar.activation(out=s_of[s][:], in_=s_of[s][:], func=ACT.Sin, scale=TWO_PI)

        def do_r(s, sine_later=False):
            r_done[s] = True
            j = s // 8
            o = 384 * j - 5 * ((384 * j) // 5)
            nc.vector.scalar_tensor_tensor(
                out=s_of[s][:],
                in0=xt[j][:, :, :, o : o + 384],
                scalar=gsc[:, s : s + 1],
                in1=kt_of[s],
                op0=ALU.mult,
                op1=ALU.subtract,
            )
            if not sine_later:
                do_sin(s)

        def do_r_third(s, kap):
            j = s // 8
            o = 384 * j - 5 * ((384 * j) // 5)
            part = s_of[s][:, :, :, kap * P : (kap + 1) * P]
            nc.vector.scalar_tensor_tensor(
                out=part,
                in0=xt[j][:, :, :, o + kap * P : o + (kap + 1) * P],
                scalar=gsc[:, s : s + 1],
                in1=kt_of[s][:, :, :, kap * P : (kap + 1) * P],
                op0=ALU.mult,
                op1=ALU.subtract,
            )
            nc.scalar.activation(out=part, in_=part, func=ACT.Sin, scale=TWO_PI)

        def do_ct(g):
            j, q = divmod(g, 24)
            m, kap = divmod(q, 3)
            ct_of[g] = psc.tile([P, 4, P], F32, name="ct")
            for dc in range(4):
                nc.tensor.transpose(ct_of[g][:, dc, :], cn[(kap, dc)][:].bitcast(F32)[:, :, (m * 5 + j) // 2], ident_f[:])

        def do_m(g):
            j, q = divmod(g, 24)
            m, kap = divmod(q, 3)
            sel = (q % 4) // 2
            h = q % 2
            if sel == 0:
                pt[h] = ppool.tile([P, 4, 4, 4, 32], F32, name="pt", align_bytes=64)
            width = 1 if g == 119 else 4
            for c in range(0, 4, width):
                nc.vector.tensor_tensor(
                    out=pt[h][:].rearrange("p c i (b s) q -> p b c i s q", b=2)[:, :, c : c + width, :, sel, :],
                    in0=s_of[j * 8 + m][:, :, c : c + width, kap * P : (kap + 1) * P].rearrange(
                        "p b c (i q) -> p b c i q", i=4
                    ),
                    in1=ct_of[g][:]
                    .bitcast(BF16)[:, c : c + width, :]
                    .rearrange("p c (i q t) -> p c i q t", i=4, t=2)[:, :, :, :, (m * 5 + j) % 2]
                    .unsqueeze(1)
                    .to_broadcast([P, 2, width, 4, 32]),
                    op=ALU.mult,
                )

        def coef_to_sbuf(g):
            j, q = divmod(g, 24)
            m = q // 3
            cur["cf"] = opool.tile([P, 4, P], BF16, name="sh", bufs=3)
            nc.scalar.copy(
                out=cur["cf"][:],
                in_=ct_of[g][:].bitcast(BF16).rearrange("p c (r t) -> p c r t", t=2)[:, :, :, (m * 5 + j) % 2],
            )

        def do_m_gpsimd(g):
            j, q = divmod(g, 24)
            m, kap = divmod(q, 3)
            sel = (q % 4) // 2
            h = q % 2
            if sel == 0:
                pt[h] = ppool.tile([P, 4, 4, 4, 32], F32, name="pt", align_bytes=64)
            nc.vector.memset(pt[h][:, 0, 0, sel : sel + 1, 0:1], 0.0)
            nc.gpsimd.tensor_tensor(
                out=pt[h][:].rearrange("p c i (b s) q -> p b c i s q", b=2)[:, :, :, :, sel, :],
                in0=s_of[j * 8 + m][:, :, :, kap * P : (kap + 1) * P].rearrange("p b c (i q) -> p b c i q", i=4),
                in1=cur["cf"][:].rearrange("p c (i q) -> p c i q", i=4).unsqueeze(1).to_broadcast([P, 2, 4, 4, 32]),
                op=ALU.mult,
            )

        def sh_turn(n):
            cts_of[n] = psc.tile([P, 4, P], BF16, name="ct")
            for dc in range(4):
                nc.tensor.transpose(cts_of[n][:, dc, :], sh_of[n][:, dc * P : (dc + 1) * P], ident_b[:])

        def sh_copy(n, k):
            def run():
                sht_of[n + k] = opool.tile([P, 4, P], F32, name="sht")
                nc.scalar.copy(
                    out=sht_of[n + k][:].rearrange("p c (b r) -> p c b r", b=2),
                    in_=cts_of[n][:, :, k * 64 : (k + 1) * 64].unsqueeze(2).to_broadcast([P, 4, 2, 64]),
                )

            return run

        def open_acc(n, pool, name):
            acc_of[n] = pool.tile([P, 512], F32, name=name)
            if n < 3:
                return
            if plain_shift(n):
                nc.tensor.matmul(out=acc_of[n][:], lhsT=ident_b[:], rhs=sh_of[n][:], start=True, stop=False)
            for dc in range(0 if plain_shift(n) else 4):
                nc.tensor.matmul(
                    out=acc_of[n][:, dc * P : (dc + 1) * P],
                    lhsT=sht_of[n][:, dc, :],
                    rhs=ident_f[:],
                    is_transpose=True,
                    start=(dc == 0),
                    stop=False,
                )

        def do_ta(n, h):
            if h == 0:
                open_acc(n, psa, "acc")
            for dc in range(4):
                for i in range(4):
                    nc.tensor.matmul(
                        out=acc_of[n][:, dc * P : (dc + 1) * P],
                        lhsT=pt[h][:, dc, i].rearrange("p a q -> p (a q)"),
                        rhs=ident_f[:],
                        is_transpose=True,
                        start=False,
                        stop=(h == 1 and dc == 3 and i == 3),
                    )

        def out_chain(n):
            t = {}
            rows = slice(n * 64, (n + 1) * 64)

            def evac():
                t["o"] = opool.tile([P, 512], F32, name="o", align_bytes=64)
                nc.scalar.copy(out=t["o"][:], in_=acc_of[n][:])
                for b in range(2):
                    nc.sync.dma_start(out=out0_v[b, rows, :], in_=t["o"][b * 64 : (b + 1) * 64, :])

            def amax():
                t["am"] = opool.tile([P, 1], F32, name="am")
                nc.vector.tensor_reduce(
                    out=t["am"][:], in_=t["o"][:], axis=AX.X, op=ALU.max, apply_absolute_value=True
                )

            def recip():
                t["rc"] = opool.tile([P, 1], F32, name="rc")
                nc.vector.reciprocal(out=t["rc"][:], in_=t["am"][:])

            def cast():
                t["rs"] = opool.tile([P, 1], F32, name="rs")
                nc.scalar.activation(out=t["rs"][:], in_=t["rc"][:], func=ACT.Copy, scale=448.0)
                t["f8"] = opool.tile([P, 512], FP8, name="f8")
                nc.scalar.activation(
                    out=t["f8"][:],
                    in_=t["o"][:],
                    func=ACT.Identity,
                    scale=t["rs"][:, 0:1],
                    bias=zero_col[:, 0:1],
                    saturate=False,
                )
                nc.sync.dma_start(out=out1_v[:, rows, :], in_=t["f8"][:].bitcast(U8))

            def cast_on_vector():
                t["rs"] = opool.tile([P, 1], F32, name="rs")
                nc.vector.tensor_scalar(out=t["rs"][:], in0=t["rc"][:], scalar1=448.0, scalar2=None, op0=ALU.mult)
                t["f8"] = opool.tile([P, 512], FP8, name="f8")
                nc.vector.tensor_scalar(
                    out=t["f8"][:], in0=t["o"][:], scalar1=t["rs"][:, 0:1], scalar2=None, op0=ALU.mult, saturate=False
                )
                nc.sync.dma_start(out=out1_v[:, rows, :], in_=t["f8"][:].bitcast(U8))

            return evac, amax, recip, cast, cast_on_vector

        def k_one(p, m, eng):
            eng.tensor_scalar(
                out=kph[p][:, :, m, :],
                in0=xt[0][:, :, p, 0:384],
                scalar1=gsc[:, m : m + 1],
                scalar2=0.0,
                op0=ALU.mult,
                op1=ALU.add,
            )

        def k_phase(p, eng, count=4):
            sph[p] = spool.tile([P, 2, 4, 384], F32, name="st")
            kph[p] = sph[p][:].bitcast(I32)
            for m in range(count):
                k_one(p, m, eng)

        def r_phase(p, half):
            for mm in range(2):
                m = 2 * half + mm
                nc.vector.scalar_tensor_tensor(
                    out=sph[p][:, :, m, :],
                    in0=xt[0][:, :, p, 0:384],
                    scalar=gsc[:, m : m + 1],
                    in1=kph[p][:, :, m, :],
                    op0=ALU.mult,
                    op1=ALU.subtract,
                )

        def sin_phase(p, half):
            part = sph[p][:, :, 2 * half : 2 * half + 2, :]
            nc.scalar.activation(out=part, in_=part, func=ACT.Sin, scale=TWO_PI)

        def ct_phase(p, n):
            cth[(p, n)] = psc.tile([P, 4, P], F32, name="ct")
            for gg in range(4):
                m, kap = divmod(4 * n + gg, 3)
                nc.tensor.transpose(cth[(p, n)][:, gg, :], cn[(kap, p)][:].bitcast(F32)[:, :, (m * 5) // 2], ident_f[:])

        def ct_last_phase(p):
            for n in range(3):
                cth[(p, n)] = psc.tile([P, 4, P], F32, name="ct")
            for last_group in (False, True):
                for n in range(3):
                    for gg in range(4):
                        m, kap = divmod(4 * n + gg, 3)
                        if (kap == 2) == last_group:
                            nc.tensor.transpose(
                                cth[(p, n)][:, gg, :], cn[(kap, p)][:].bitcast(F32)[:, :, (m * 5) // 2], ident_f[:]
                            )

        def m_phase(p, n):
            pth[n] = ppool.tile([P, 8, 4, 32], F32, name="pt", align_bytes=64)
            flat = sph[p][:].rearrange("p b m c -> p b (m c)")
            halves = cth[(p, n)][:].bitcast(BF16).rearrange("p h (i q t) -> p h i q t", q=32, t=2)
            for sel in range(2):
                g0 = 4 * n + 2 * sel
                width = 2 if (g0 // 3) % 2 == ((g0 + 1) // 3) % 2 else 1
                for h in range(0, 2, width):
                    nc.vector.tensor_tensor(
                        out=pth[n][:].rearrange("p e (b s) q -> p b e s q", b=2)[:, :, 4 * h : 4 * (h + width), sel, :],
                        in0=flat[:, :, (g0 + h) * P : (g0 + h + width) * P].rearrange("p b (e q) -> p b e q", q=32),
                        in1=halves[:, 2 * sel + h : 2 * sel + h + width, :, :, ((g0 + h) // 3) % 2]
                        .rearrange("p h i q -> p (h i) q")
                        .unsqueeze(1)
                        .to_broadcast([P, 2, 4 * width, 32]),
                        op=ALU.mult,
                    )

        def ta_phase(p, n):
            for e in range(8):
                nc.tensor.matmul(
                    out=acc_of[n][:, p * P : (p + 1) * P],
                    lhsT=pth[n][:, e].rearrange("p a q -> p (a q)"),
                    rhs=ident_f[:],
                    is_transpose=True,
                    start=(p == 0 and e == 0),
                    stop=False,
                )
            if p == 3:
                nc.tensor.matmul(out=acc_of[n][:], lhsT=ident_b[:], rhs=sh_of[n][:], start=False, stop=True)

        tp = {}
        tp[0] = turn(psc, "ct", w_words(0), w_words(1))
        tp_x = turn(psc, "ct", x_words(0), x_words(3))
        tp[1] = turn(psc, "ct", w_words(2), w_words(3))
        tp[2] = turn(psc, "ct", w_words(4), w_words(5))
        c0 = chunk(512)
        empty(tp[0], c0, 0, False)
        gxa = chunk(256)
        empty(tp_x, gxa, 0, True)
        quant(gxa, 0, 128, xc, xs, 0)
        quant(gxa, 128, 256, xc, xs, 384)
        empty(tp[1], c0, 256, False)
        quant(c0, 0, 512, wc, ws, 0)
        c1 = chunk(256)
        empty(tp[2], c1, 0, False)
        quant(c1, 0, 256, wc, ws, 512)
        tb = psc.tile([P, P], BF16, name="ct")
        nc.tensor.transpose(tb[:], lb[:], ident_b[:])
        nc.vector.tensor_copy(out=bias_t[:], in_=tb[:, 0:20])
        gp = psc.tile([P, 40], F32, name="ct")
        nc.tensor.matmul(out=gp[:], lhsT=first_row[:], rhs=g_row[:], start=True, stop=True)
        nc.vector.tensor_scalar(out=gsc[:], in0=gp[:], scalar1=1.0 / TWO_PI, scalar2=None, op0=ALU.mult)
        tp[3] = turn(psc, "ct", w_words(6), w_words(7))
        tp[4] = turn(psc, "ct", w_words(8), w_words(9))
        xmm(0, 0)
        xmm(0, 1)
        c2 = chunk(512)
        empty(tp[3], c2, 0, False)
        empty(tp[4], c2, 256, True)
        xev_unit(0, 0, False, True)
        xev_unit(0, 1, True, True)
        xev_unit(0, 2, False, True)
        xev_unit(0, 3, True, True)
        xmm(0, 2)
        quant(c2, 0, 512, wc, ws, 768)
        tp[5] = turn(psc, "ct", w_words(10), w_words(11))
        tp[6] = turn(psc, "ct", w_words(12), w_words(13))
        xev_unit(0, 4, False, True)
        xev_unit(0, 5, False, True)
        xmm(0, 3)
        xmm(0, 4)
        k_phase(0, nc.vector)
        for beta in range(6, 10):
            xev_unit(0, beta, False, False)
        r_phase(0, 0)
        c3 = chunk(512)
        empty(tp[5], c3, 0, False)
        empty(tp[6], c3, 256, False)
        r_phase(0, 1)
        for i in range(7, 10):
            tp[i] = turn(psc, "ct", w_words(2 * i), w_words(2 * i + 1))
        sin_phase(0, 0)
        c4 = chunk(512)
        empty(tp[7], c4, 0, False)
        empty(tp[8], c4, 256, False)
        quant(c3, 0, 512, wc, ws, 1280)
        quant(c4, 0, 512, wc, ws, 1792)
        sin_phase(0, 1)
        xmm(0, 5)
        xmm(0, 6)
        k_phase(1, nc.vector)
        for beta in range(10, 14):
            xev_unit(0, beta, False, False)
        xmm(0, 7)
        xev_unit(0, 14, False, False)
        xev_unit(0, 15, False, False)
        r_phase(1, 0)
        r_phase(1, 1)
        c5 = chunk(256)
        empty(tp[9], c5, 0, False)
        for n in range(3):
            ct_phase(0, n)
        open_acc(0, psa, "acc")
        open_acc(1, psa, "acc")
        open_acc(2, psc, "ct")
        sin_phase(1, 0)
        sin_phase(1, 1)
        quant(c5, 0, 256, wc, ws, 2304)
        xmm(0, 8)
        xev_unit(0, 16, False, False)
        xev_unit(0, 17, False, False)
        xmm(0, 9)
        xev_unit(0, 18, False, False)
        xev_unit(0, 19, False, False)
        tp_y = turn(psc, "ct", x_words(1), x_words(2))
        tp_z = turn(psc, "ct", x_words(4), x_words(5))
        for kap in range(3):
            load_coef(kap, 3, "late%d" % kap)
        for n in range(6):
            sh_load(n)
        gxb = opool.tile([P, 256, 4], BF16, name="o", align_bytes=64)
        empty(tp_y, gxb, 0, False)
        gxc = opool.tile([P, 256, 4], BF16, name="o", align_bytes=64)
        empty(tp_z, gxc, 0, False)

        chains = {}
        xevs = []
        for p in range(HEAD):
            if p == 3:
                xevs = [xev_later(1, 5)]
                xev_unit(1, 8, True, False)
                xev_unit(1, 9, True, False)
            for fn in xevs:
                fn()
            xevs = []
            if p < 2:
                k_phase(p + 2, nc.gpsimd, 3)
            elif p == 2:
                do_k(p + 2)
            for n in range(3):
                m_phase(p, n)
                ta_phase(p, n)
                if p < 2:
                    ct_phase(p + 1, n)
                elif p == 3:
                    chains[n] = out_chain(n)
                    if n < 2:
                        do_ct(3 * HEAD + n)
                    if n >= 1:
                        chains[n - 1][0]()
            if p < 2:
                r_phase(p + 2, 0)
                sin_phase(p + 2, 0)
                k_one(p + 2, 3, nc.vector)
                r_phase(p + 2, 1)
                sin_phase(p + 2, 1)
            elif p == 2:
                do_k(HEAD + 1)
                do_r(HEAD)
            else:
                do_r(HEAD + 1, True)
                chains[0][1]()
                chains[0][2]()
                for fn in xevs:
                    fn()
                xevs = []
            if p == 0:
                quant(gxb, 0, 256, xc, xs, 128)
                quant(gxc, 0, 256, xc, xs, 512)
            for t in (2 * p, 2 * p + 1):
                xmm(1, t)
                xevs.extend([xev_later(1, t, p == 2)])
            if p == 2:
                ct_last_phase(3)

        x_units = {HEAD: [(1, 8), (1, 9)]}
        for grp in range(2, 5):
            for t in range(10):
                x_units.setdefault(8 * grp - 10 + (7 * t) // 10, []).extend([(grp, t)])
        casts = [chains[0][3]]
        late_casts = [chains[1][3]]
        evacs = [chains[2]]
        copies = []
        copies_later = []
        dve_small = [chains[1][1], chains[1][2]]
        for s in range(HEAD, 39):
            j, m = divmod(s, 8)
            if s == HEAD:
                for fn in copies + xevs:
                    fn()
            for fn in casts:
                fn()
            new_small = []
            for fns in evacs:
                fns[0]()
                new_small.extend([fns[1], fns[2]])
            cast_next = late_casts + [fns[3] for fns in evacs]
            late_casts = []
            if s > HEAD:
                for fn in copies + xevs:
                    fn()
            casts = cast_next
            evacs = []
            copies = copies_later
            copies_later = []
            xevs = []
            dve_small.extend(new_small)
            if s == HEAD:
                do_sin(HEAD + 1)
            if s + 1 < 39 and s + 1 not in r_done:
                do_r(s + 1)
            if s + 2 < 40 and (s + 2, 0) not in kt_of:
                do_k(s + 2)
            for kap in range(3 if s < 38 else 0):
                g = 3 * s + kap
                if g + 2 < 120:
                    do_ct(g + 2)
                if (g - 1) % 4 >= 2 and (g - 1) // 4 >= 3:
                    do_ta((g - 1) // 4, (g - 1) % 2)
                    if (g - 1) % 4 == 3:
                        evacs.extend([out_chain((g - 1) // 4)])
                if g % 4 == 0 and pair_start(g // 4 + 1):
                    sh_turn(g // 4 + 1)
                    copies.extend([sh_copy(g // 4 + 1, 0)])
                    copies_later.extend([sh_copy(g // 4 + 1, 1)])
                if g % 4 == 0 and 6 <= g // 4 + 2 < 30 and (plain_shift(g // 4 + 2) or pair_start(g // 4 + 2)):
                    sh_load(g // 4 + 2)
                do_m(g)
                take = 0 if kap == 2 else ((len(dve_small) + 1) // 2 if kap == 0 else len(dve_small))
                for fn in dve_small[:take]:
                    fn()
                dve_small = dve_small[take:]
            for grp, t in x_units.get(s, []):
                xmm(grp, t)
                xevs.extend([xev_later(grp, t)])
        do_ct(116)
        do_ct(118)
        coef_to_sbuf(116)
        do_m(114)
        do_r_third(39, 1)
        do_ta(28, 0)
        do_m_gpsimd(116)
        do_ct(117)
        do_m(115)
        for fn in dve_small:
            fn()
        do_ta(28, 1)
        before_last = out_chain(28)
        do_ct(119)
        for fn in casts:
            fn()
        do_m(118)
        do_ta(29, 0)
        do_r_third(39, 0)
        do_r_third(39, 2)
        before_last[0]()
        do_m(117)
        do_m(119)
        do_ta(29, 1)
        before_last[1]()
        before_last[2]()
        last = out_chain(29)
        last[0]()
        before_last[3]()
        last[1]()
        last[2]()
        last[4]()
